import numpy as np
import ml_dtypes


def mxq(x, axis, fmt="e4m3"):
    dtype, down = {"e4m3": (ml_dtypes.float8_e4m3fn, 7), "e5m2": (ml_dtypes.float8_e5m2, 14)}[fmt]
    v = np.moveaxis(np.asarray(x, np.float32).astype(ml_dtypes.bfloat16).astype(np.float64), axis, -1)
    blocks = v.reshape(v.shape[:-1] + (-1, 32))
    amax = np.abs(blocks).max(-1, keepdims=True)
    byte = np.maximum(np.where(amax > 0, np.frexp(amax)[1] - 1 + 127, 0) - down, 1)
    scale = np.exp2(byte - 127.0)
    codes = (blocks / scale).astype(np.float32).astype(dtype).astype(np.float64)
    return np.moveaxis((codes * scale).reshape(v.shape), -1, axis)


WIDE = False


def mx_kscale(k):
    if not WIDE:
        return np.ones(k)
    levels = np.array([10, -10, 5, -5, 0])
    a = np.random.permutation(np.resize(levels, k // 512 * 4)).reshape(k // 512, 4)
    idx = np.arange(k)
    return np.exp2(a[idx // 512, idx % 128 // 32])


BF16 = ml_dtypes.bfloat16


def bf(x):
    return np.asarray(x, np.float32).astype(BF16)


def f64(x):
    return np.asarray(x).astype(np.float64)


N, E, SD, AD, RD, HID, NH = 4096, 3, 120, 8, 8, 512, 3
OD = SD + RD


def swish(v):
    return v * (1.0 / (1.0 + np.exp(-v)))


def softplus(v):
    return np.maximum(v, 0.0) + np.log1p(np.exp(-np.abs(v)))


def soft_clamp_exp(v, hi, lo):
    v = (hi - softplus(hi - 2.0 * v)) / 2.0
    v = (lo + softplus(2.0 * v - lo)) / 2.0
    return np.exp(v)


def setup_inputs():
    ks = mx_kscale(HID)
    return {"h": bf(swish(np.random.standard_normal((N, E, HID))) * ks),
            "Wh": bf(np.random.standard_normal((E, HID, HID)) * 1.6 / np.sqrt(HID) / ks[None, :, None]),
            "bh": bf(np.random.standard_normal((E, HID)) * 0.2),
            "Wmu": bf(np.random.standard_normal((E, HID, OD)) * 1.6 / np.sqrt(HID)),
            "bmu": bf(np.random.standard_normal((E, OD)) * 0.3),
            "Wsig": bf(np.random.standard_normal((E, HID, OD)) * 2.0 / np.sqrt(HID)),
            "bsig": bf(np.random.standard_normal((E, OD)) * 0.3),
            "max_lv_s": bf(0.5 + 0.2 * np.random.standard_normal((1, SD))),
            "min_lv_s": bf(-2.5 + 0.3 * np.random.standard_normal((1, SD))),
            "max_lv_r": bf(0.5 + 0.2 * np.random.standard_normal((1, RD))),
            "min_lv_r": bf(-2.5 + 0.3 * np.random.standard_normal((1, RD)))}


def reference(h, Wh, bh, Wmu, bmu, Wsig, bsig, max_lv_s, min_lv_s, max_lv_r, min_lv_r):
    hq = mxq(f64(h), 2, "e4m3").transpose(1, 0, 2)
    g = swish((hq @ mxq(f64(Wh), 1, "e4m3")) + f64(bh)[:, None, :])
    gq = mxq(g, 2, "e4m3")
    mu = ((gq @ mxq(f64(Wmu), 1, "e4m3")) + f64(bmu)[:, None, :]).transpose(1, 0, 2)
    sigma = ((gq @ mxq(f64(Wsig), 1, "e4m3")) + f64(bsig)[:, None, :]).transpose(1, 0, 2)
    ds_mu, r_mu = mu[..., :SD], mu[..., SD:]
    ds_sg, r_sg = sigma[..., :SD], sigma[..., SD:]
    ds_sg = soft_clamp_exp(ds_sg, f64(max_lv_s), f64(min_lv_s))
    r_sg = soft_clamp_exp(r_sg, f64(max_lv_r), f64(min_lv_r))
    return ds_mu, ds_sg, r_mu, r_sg

@@ -1,0 +1,286 @@
+from contextlib import ExitStack
+
+import concourse.mybir as mybir
+from concourse.masks import make_identity
+
+F32 = mybir.dt.float32
+BF16 = mybir.dt.bfloat16
+U32 = mybir.dt.uint32
+U8 = mybir.dt.uint8
+FP8X4 = mybir.dt.float8_e4m3fn_x4
+ACT = mybir.ActivationFunctionType
+ALU = mybir.AluOpType
+
+N, E, HID, OD, SD = 4096, 3, 512, 128, 120
+P = 128
+CH = 8
+SL = 4
+NIT = CH * E
+FLOPS = 2 * N * E * HID * (HID + 2 * OD)
+MANUAL = True
+
+
+def tile_ensembleenvprob_pa_t_kernel(
+    tc, h, Wh, bh, Wmu, bmu, Wsig, bsig, max_lv_s, min_lv_s, max_lv_r, min_lv_r,
+    out_0, out_1, out_2, out_3,
+):
+    nc = tc.nc
+    with ExitStack() as ctx:
+        const = ctx.enter_context(tc.tile_pool(name="const", bufs=1))
+        keep = ctx.enter_context(tc.tile_pool(name="keep", bufs=1))
+        big = ctx.enter_context(tc.tile_pool(name="big", bufs=4))
+        work = ctx.enter_context(tc.tile_pool(name="work", bufs=3))
+        psum = ctx.enter_context(tc.psum_pool(name="psum", bufs=1))
+        if MANUAL:
+            ctx.enter_context(tc.manual_schedule())
+
+        h_rows = h.rearrange("(p c t) e k -> c p (t e k)", c=CH, t=SL)
+        h_by_e = h.rearrange("(p c t) e k -> c e p t k", c=CH, t=SL)
+        ds_mu_rows = out_0.rearrange("(p c t) e o -> c p (t e o)", c=CH, t=SL)
+        ds_sg_rows = out_1.rearrange("(p c t) e o -> c p (t e o)", c=CH, t=SL)
+        r_mu_rows = out_2.rearrange("(p c t) e o -> p (c t e o)", c=CH, t=SL)
+        r_sg_rows = out_3.rearrange("(p c t) e o -> p (c t e o)", c=CH, t=SL)
+
+        ident_f = const.tile([P, P], F32, name="ident_f")
+        make_identity(nc, ident_f[:])
+        ident_b = const.tile([P, P], BF16, name="ident_b")
+        make_identity(nc, ident_b[:])
+        vecs = const.tile([P, P], BF16, name="vecs")
+        nc.vector.memset(vecs[:], 0.0)
+        nc.scalar.dma_start(out=vecs[0:12, :], in_=bh.rearrange("e (j p) -> (e j) p", p=P))
+        nc.scalar.dma_start(out=vecs[12:15, :], in_=bsig)
+        nc.scalar.dma_start(out=vecs[15:16, 0:SD], in_=max_lv_s)
+        nc.scalar.dma_start(out=vecs[16:17, 0:SD], in_=min_lv_s)
+        nc.scalar.dma_start(out=vecs[17:18, SD:OD], in_=max_lv_r)
+        nc.scalar.dma_start(out=vecs[18:19, SD:OD], in_=min_lv_r)
+
+        whq = const.tile([P, E, HID], U32, name="whq", align_bytes=64)
+        whs = const.tile([P, E, HID], U8, name="whs", align_bytes=64)
+        w2q = const.tile([P, E, 2 * OD], U32, name="w2q", align_bytes=64)
+        w2s = const.tile([P, E, 2 * OD], U8, name="w2s", align_bytes=64)
+        r_mu = const.tile([P, CH, SL, E, OD - SD], F32, name="r_mu")
+        r_sg = const.tile([P, CH, SL, E, OD - SD], F32, name="r_sg")
+        bmu_b = const.tile([P, E * OD], BF16, name="bmu_b")
+        bmu_f = const.tile([P, E * OD], F32, name="bmu_f")
+
+        h_tiles = {}
+        h_tiles[0] = big.tile([P, SL * E * HID], BF16, name="h_sb", tag="big")
+        wh_raw = big.tile([P, E, 4, HID], BF16, name="wh_raw", tag="big")
+        h0_view = h_tiles[0][:].rearrange("p (t e k) -> p t e k", t=SL, e=E)
+        for e in range(E):
+            nc.sync.dma_start(out=h0_view[:, :, e, :], in_=h_by_e[0, e])
+            nc.sync.dma_start(
+                out=wh_raw[:, e].rearrange("p (u a) f -> p u (a f)", u=2),
+                in_=Wh[e].rearrange("(u p a) f -> p u (a f)", u=2, a=2),
+            )
+        h_tiles[1] = big.tile([P, SL * E * HID], BF16, name="h_sb", tag="big")
+        nc.sync.dma_start(out=h_tiles[1][:], in_=h_rows[1])
+        w2_raw = big.tile([P, 2, E * 4, OD], BF16, name="w2_raw", tag="big")
+        nc.sync.dma_start(out=w2_raw[:, 0], in_=Wmu.rearrange("e (j p) o -> p (e j) o", p=P))
+        nc.sync.dma_start(out=w2_raw[:, 1], in_=Wsig.rearrange("e (j p) o -> p (e j) o", p=P))
+        nc.sync.dma_start(out=bmu_b[:], in_=bmu.rearrange("e o -> (e o)").partition_broadcast(P))
+
+        pv = psum.tile([P, P], BF16, name="pv", tag="b7")
+        nc.tensor.transpose(pv[:], vecs[:], ident_b[:])
+        cols = const.tile([P, 19], F32, name="cols")
+        nc.vector.tensor_copy(out=cols[:], in_=pv[:, 0:19])
+        hl = const.tile([P, 2], F32, name="hl")
+        nc.vector.tensor_tensor(out=hl[:], in0=cols[:, 15:17], in1=cols[:, 17:19], op=ALU.add)
+        c2 = const.tile([P, E], F32, name="c2")
+        nc.vector.tensor_scalar(
+            out=c2[:], in0=cols[:, 12:15], scalar1=2.0, scalar2=hl[:, 0:1],
+            op0=ALU.mult, op1=ALU.subtract,
+        )
+        ab = const.tile([P, 2], F32, name="ab")
+        nc.scalar.activation(out=ab[:], in_=hl[:], func=ACT.Exp)
+
+        def regroup(dst, src):
+            nc.vector.tensor_copy(
+                out=dst.rearrange("p (c i t) -> p c t i", i=4, t=4),
+                in_=src.rearrange("p t (c i) -> p c t i", i=4),
+            )
+
+        wgrp = {}
+
+        def wh_regroup(e):
+            wgrp[e] = work.tile([P, 4 * HID], BF16, name="whgrp", tag="ggrp", align_bytes=64)
+            regroup(wgrp[e][:], wh_raw[:, e])
+
+        def wh_quant(e):
+            nc.vector.quantize_mx(
+                out=whq[:, e, :].bitcast(FP8X4), scales=whs[:, e, :], in_=wgrp[e][:]
+            )
+
+        def w2_regroup(e):
+            wgrp[E + e] = work.tile([P, 8 * OD], BF16, name="w2grp", tag="ggrp", align_bytes=64)
+            for m in range(2):
+                regroup(
+                    wgrp[E + e][:, m * 4 * OD : (m + 1) * 4 * OD],
+                    w2_raw[:, m, 4 * e : 4 * e + 4, :],
+                )
+
+        def w2_quant(e):
+            nc.vector.quantize_mx(
+                out=w2q[:, e, :].bitcast(FP8X4), scales=w2s[:, e, :], in_=wgrp[E + e][:]
+            )
+
+        xt, hgrp, hq, hs, m1, gpl, ggrp, gq, gs, sg = {}, {}, {}, {}, {}, {}, {}, {}, {}, {}
+
+        def transposes(i):
+            c, e = divmod(i, E)
+            words = h_tiles[c][:].bitcast(F32)
+            xt[i] = []
+            for half in range(2):
+                x = psum.tile([P, 2, 2 * P], F32, name="x", tag="b%d" % (2 * (i % 2) + half))
+                for tt in range(2):
+                    base = ((2 * half + tt) * E + e) * (HID // 2)
+                    for u in range(2):
+                        nc.tensor.transpose(
+                            x[:, u, tt * P : (tt + 1) * P],
+                            words[:, base + u * P : base + (u + 1) * P],
+                            ident_f[:],
+                        )
+                xt[i].append(x)
+
+        def exits(i):
+            hgrp[i] = work.tile([P, 2 * HID], F32, name="hgrp", tag="hgrp", align_bytes=64)
+            for half in range(2):
+                dst = hgrp[i][:, half * HID : (half + 1) * HID].rearrange("p (n u) -> p n u", u=2)
+                src = xt[i][half][:].rearrange("p u n -> p n u")
+                if half == 0:
+                    nc.scalar.copy(out=dst, in_=src)
+                else:
+                    nc.vector.tensor_copy(out=dst, in_=src)
+
+        def quant_h(i):
+            hq[i] = work.tile([P, HID], U32, name="hq", tag="hq", align_bytes=64)
+            hs[i] = work.tile([P, HID], U8, name="hs", tag="hs", align_bytes=64)
+            nc.vector.quantize_mx(
+                out=hq[i][:].bitcast(FP8X4), scales=hs[i][:], in_=hgrp[i][:].bitcast(BF16)
+            )
+
+        def stage1(i):
+            e = i % E
+            m1[i] = []
+            for j in range(4):
+                acc = psum.tile([P, HID], F32, name="acc", tag="b%d" % (4 + j))
+                nc.tensor.matmul_mx(
+                    out=acc[:],
+                    lhsT=whq[:, e, j * P : (j + 1) * P].bitcast(FP8X4),
+                    lhsT_scale=whs[:, e, j * P : (j + 1) * P],
+                    rhs=hq[i][:].bitcast(FP8X4),
+                    rhs_scale=hs[i][:],
+                    start=True,
+                    stop=True,
+                )
+                m1[i].append(acc)
+
+        def silu(i):
+            e = i % E
+            gpl[i] = work.tile([P, 4, HID], BF16, name="gpl", tag="gpl")
+            for j in range(4):
+                nc.scalar.activation(
+                    out=gpl[i][:, j, :], in_=m1[i][j][:], func=ACT.Silu,
+                    bias=cols[:, 4 * e + j : 4 * e + j + 1], scale=1.0,
+                )
+
+        def regroup_g(i):
+            ggrp[i] = work.tile([P, 4 * HID], BF16, name="ggrp", tag="ggrp", align_bytes=64)
+            regroup(ggrp[i][:], gpl[i][:])
+
+        def quant_g(i):
+            gq[i] = keep.tile([P, HID], U32, name="gq%d" % i, align_bytes=64)
+            gs[i] = keep.tile([P, HID], U8, name="gs%d" % i, align_bytes=64)
+            nc.vector.quantize_mx(out=gq[i][:].bitcast(FP8X4), scales=gs[i][:], in_=ggrp[i][:])
+
+        wh_regroup(0)
+        for tick in range(-2, NIT + 2):
+            if tick >= 0 and tick % E == 0 and tick // E + 2 < CH:
+                c = tick // E + 2
+                h_tiles[c] = big.tile([P, SL * E * HID], BF16, name="h_sb", tag="big")
+                nc.sync.dma_start(out=h_tiles[c][:], in_=h_rows[c])
+            if tick + 2 < NIT:
+                transposes(tick + 2)
+            if 0 <= tick - 1 < NIT:
+                regroup_g(tick - 1)
+            if 0 <= tick < NIT:
+                silu(tick)
+            if 0 <= tick + 1 < NIT:
+                quant_h(tick + 1)
+                stage1(tick + 1)
+            if 0 <= tick - 1 < NIT:
+                quant_g(tick - 1)
+            if tick == -2:
+                wh_quant(0)
+            if tick in (-1, 0):
+                wh_quant(tick + 2)
+            if tick in (1, 2, 3):
+                w2_quant(tick - 1)
+            if tick + 2 < NIT:
+                exits(tick + 2)
+            if tick in (-2, -1):
+                wh_regroup(tick + 3)
+            if tick in (0, 1, 2):
+                w2_regroup(tick)
+            if tick == 3:
+                nc.vector.tensor_copy(out=bmu_f[:], in_=bmu_b[:])
+
+        ds = {}
+        for i in range(NIT):
+            c, e = divmod(i, E)
+            pm = psum.tile([P, SL, OD], F32, name="pm", tag="b%d" % (i % 4))
+            for t in range(SL):
+                nc.tensor.matmul_mx(
+                    out=pm[:, t, :],
+                    lhsT=gq[i][:, t * P : (t + 1) * P].bitcast(FP8X4),
+                    lhsT_scale=gs[i][:, t * P : (t + 1) * P],
+                    rhs=w2q[:, e, 0:OD].bitcast(FP8X4),
+                    rhs_scale=w2s[:, e, 0:OD],
+                    start=True,
+                    stop=True,
+                )
+            pg = psum.tile([P, HID], F32, name="pg", tag="b%d" % (4 + i % 4))
+            nc.tensor.matmul_mx(
+                out=pg[:],
+                lhsT=w2q[:, e, OD : 2 * OD].bitcast(FP8X4),
+                lhsT_scale=w2s[:, e, OD : 2 * OD],
+                rhs=gq[i][:].bitcast(FP8X4),
+                rhs_scale=gs[i][:],
+                start=True,
+                stop=True,
+            )
+            sg[i] = keep.tile([P, HID], F32, name="sg%d" % i)
+            nc.scalar.activation(
+                out=sg[i][:], in_=pg[:], func=ACT.Sigmoid, bias=c2[:, e : e + 1], scale=2.0
+            )
+            if e == 0:
+                ds[c] = big.tile([P, SL, E, SD], F32, name="ds_mu", tag="big")
+            nc.vector.tensor_tensor(
+                out=ds[c][:, :, e, :], in0=pm[:, :, 0:SD],
+                in1=bmu_f[:, e * OD : e * OD + SD].unsqueeze(1).to_broadcast([P, SL, SD]),
+                op=ALU.add,
+            )
+            nc.vector.tensor_tensor(
+                out=r_mu[:, c, :, e, :], in0=pm[:, :, SD:OD],
+                in1=bmu_f[:, e * OD + SD : (e + 1) * OD].unsqueeze(1).to_broadcast([P, SL, OD - SD]),
+                op=ALU.add,
+            )
+            if e == E - 1:
+                nc.sync.dma_start(out=ds_mu_rows[c], in_=ds[c][:].rearrange("p t e o -> p (t e o)"))
+        nc.sync.dma_start(out=r_mu_rows, in_=r_mu[:].rearrange("p c t e o -> p (c t e o)"))
+
+        for i in range(NIT):
+            c, e = divmod(i, E)
+            nc.scalar.activation(
+                out=sg[i][:], in_=sg[i][:], func=ACT.Sqrt, bias=ab[:, 1:2], scale=ab[:, 0:1]
+            )
+            pt = psum.tile([P, SL, OD], F32, name="pt", tag="b%d" % (i % 8))
+            for t in range(SL):
+                nc.tensor.transpose(pt[:, t, :], sg[i][:, t * P : (t + 1) * P], ident_f[:])
+            if e == 0:
+                ds[c] = big.tile([P, SL, E, SD], F32, name="ds_sg", tag="big")
+            nc.vector.tensor_copy(out=ds[c][:, :, e, :], in_=pt[:, :, 0:SD])
+            nc.vector.tensor_copy(out=r_sg[:, c, :, e, :], in_=pt[:, :, SD:OD])
+            if e == E - 1:
+                nc.sync.dma_start(out=ds_sg_rows[c], in_=ds[c][:].rearrange("p t e o -> p (t e o)"))
+        nc.sync.dma_start(out=r_sg_rows, in_=r_sg[:].rearrange("p c t e o -> p (c t e o)"))

@@ -18,6 +18,7 @@ SL = 4
 NIT = CH * E
 FLOPS = 2 * N * E * HID * (HID + 2 * OD)
 MANUAL = True
+SCALAR_TAKES_BOTH = 5
 
 
 def tile_ensembleenvprob_pa_t_kernel(
@@ -28,18 +29,17 @@ def tile_ensembleenvprob_pa_t_kernel(
     with ExitStack() as ctx:
         const = ctx.enter_context(tc.tile_pool(name="const", bufs=1))
         keep = ctx.enter_context(tc.tile_pool(name="keep", bufs=1))
-        big = ctx.enter_context(tc.tile_pool(name="big", bufs=4))
+        io = ctx.enter_context(tc.tile_pool(name="io", bufs=9))
         work = ctx.enter_context(tc.tile_pool(name="work", bufs=3))
         psum = ctx.enter_context(tc.psum_pool(name="psum", bufs=1))
         if MANUAL:
             ctx.enter_context(tc.manual_schedule())
 
-        h_rows = h.rearrange("(p c t) e k -> c p (t e k)", c=CH, t=SL)
         h_by_e = h.rearrange("(p c t) e k -> c e p t k", c=CH, t=SL)
-        ds_mu_rows = out_0.rearrange("(p c t) e o -> c p (t e o)", c=CH, t=SL)
-        ds_sg_rows = out_1.rearrange("(p c t) e o -> c p (t e o)", c=CH, t=SL)
-        r_mu_rows = out_2.rearrange("(p c t) e o -> p (c t e o)", c=CH, t=SL)
-        r_sg_rows = out_3.rearrange("(p c t) e o -> p (c t e o)", c=CH, t=SL)
+        ds_mu_rows = out_0.rearrange("(p c t) e o -> c p t (e o)", c=CH, t=SL)
+        ds_sg_rows = out_1.rearrange("(p c t) e o -> c p t (e o)", c=CH, t=SL)
+        r_mu_rows = out_2.rearrange("(p c t) e o -> p c (t e o)", c=CH, t=SL)
+        r_sg_rows = out_3.rearrange("(p c t) e o -> p c (t e o)", c=CH, t=SL)
 
         ident_f = const.tile([P, P], F32, name="ident_f")
         make_identity(nc, ident_f[:])
@@ -48,11 +48,12 @@ def tile_ensembleenvprob_pa_t_kernel(
         vecs = const.tile([P, P], BF16, name="vecs")
         nc.vector.memset(vecs[:], 0.0)
         nc.scalar.dma_start(out=vecs[0:12, :], in_=bh.rearrange("e (j p) -> (e j) p", p=P))
-        nc.scalar.dma_start(out=vecs[12:15, :], in_=bsig)
         nc.scalar.dma_start(out=vecs[15:16, 0:SD], in_=max_lv_s)
         nc.scalar.dma_start(out=vecs[16:17, 0:SD], in_=min_lv_s)
         nc.scalar.dma_start(out=vecs[17:18, SD:OD], in_=max_lv_r)
         nc.scalar.dma_start(out=vecs[18:19, SD:OD], in_=min_lv_r)
+        vecs2 = const.tile([P, P], BF16, name="vecs2")
+        nc.vector.memset(vecs2[:], 0.0)
 
         whq = const.tile([P, E, HID], U32, name="whq", align_bytes=64)
         whs = const.tile([P, E, HID], U8, name="whs", align_bytes=64)
@@ -62,37 +63,42 @@ def tile_ensembleenvprob_pa_t_kernel(
         r_sg = const.tile([P, CH, SL, E, OD - SD], F32, name="r_sg")
         bmu_b = const.tile([P, E * OD], BF16, name="bmu_b")
         bmu_f = const.tile([P, E * OD], F32, name="bmu_f")
+        cols = const.tile([P, 19], F32, name="cols")
+        cols2 = const.tile([P, E], F32, name="cols2")
+        hl = const.tile([P, 2], F32, name="hl")
+        c2 = const.tile([P, E], F32, name="c2")
+        ab = const.tile([P, 2], F32, name="ab")
 
-        h_tiles = {}
-        h_tiles[0] = big.tile([P, SL * E * HID], BF16, name="h_sb", tag="big")
-        wh_raw = big.tile([P, E, 4, HID], BF16, name="wh_raw", tag="big")
-        h0_view = h_tiles[0][:].rearrange("p (t e k) -> p t e k", t=SL, e=E)
-        for e in range(E):
-            nc.sync.dma_start(out=h0_view[:, :, e, :], in_=h_by_e[0, e])
+        h_tiles, wh_raw, w2_raw, wgrp = {}, {}, {}, {}
+        xt, hgrp, hq, hs, m1, gpl, ggrp, gq, gs, sg, ds = {}, {}, {}, {}, {}, {}, {}, {}, {}, {}, {}
+
+        def ce(i):
+            return i % CH, i // CH
+
+        def load_h(i, pieces=1):
+            c, e = ce(i)
+            h_tiles[i] = io.tile([P, SL * HID], BF16, name="h_sb", tag="io")
+            view = h_tiles[i][:].rearrange("p (t k) -> p t k", t=SL)
+            step = SL // pieces
+            for s in range(pieces):
+                nc.sync.dma_start(
+                    out=view[:, s * step : (s + 1) * step, :],
+                    in_=h_by_e[c, e][:, s * step : (s + 1) * step, :],
+                )
+
+        def load_wh(e):
+            wh_raw[e] = io.tile([P, 4, HID], BF16, name="wh_raw", tag="io")
             nc.sync.dma_start(
-                out=wh_raw[:, e].rearrange("p (u a) f -> p u (a f)", u=2),
+                out=wh_raw[e][:].rearrange("p (u a) f -> p u (a f)", u=2),
                 in_=Wh[e].rearrange("(u p a) f -> p u (a f)", u=2, a=2),
             )
-        h_tiles[1] = big.tile([P, SL * E * HID], BF16, name="h_sb", tag="big")
-        nc.sync.dma_start(out=h_tiles[1][:], in_=h_rows[1])
-        w2_raw = big.tile([P, 2, E * 4, OD], BF16, name="w2_raw", tag="big")
-        nc.sync.dma_start(out=w2_raw[:, 0], in_=Wmu.rearrange("e (j p) o -> p (e j) o", p=P))
-        nc.sync.dma_start(out=w2_raw[:, 1], in_=Wsig.rearrange("e (j p) o -> p (e j) o", p=P))
-        nc.sync.dma_start(out=bmu_b[:], in_=bmu.rearrange("e o -> (e o)").partition_broadcast(P))
 
-        pv = psum.tile([P, P], BF16, name="pv", tag="b7")
-        nc.tensor.transpose(pv[:], vecs[:], ident_b[:])
-        cols = const.tile([P, 19], F32, name="cols")
-        nc.vector.tensor_copy(out=cols[:], in_=pv[:, 0:19])
-        hl = const.tile([P, 2], F32, name="hl")
-        nc.vector.tensor_tensor(out=hl[:], in0=cols[:, 15:17], in1=cols[:, 17:19], op=ALU.add)
-        c2 = const.tile([P, E], F32, name="c2")
-        nc.vector.tensor_scalar(
-            out=c2[:], in0=cols[:, 12:15], scalar1=2.0, scalar2=hl[:, 0:1],
-            op0=ALU.mult, op1=ALU.subtract,
-        )
-        ab = const.tile([P, 2], F32, name="ab")
-        nc.scalar.activation(out=ab[:], in_=hl[:], func=ACT.Exp)
+        def load_w2():
+            for m, w in enumerate((Wmu, Wsig)):
+                w2_raw[m] = io.tile([P, E * 4, OD], BF16, name="w2_raw", tag="io")
+                nc.sync.dma_start(out=w2_raw[m][:], in_=w.rearrange("e (j p) o -> p (e j) o", p=P))
+            nc.sync.dma_start(out=bmu_b[:], in_=bmu.rearrange("e o -> (e o)").partition_broadcast(P))
+            nc.sync.dma_start(out=vecs2[0:E, :], in_=bsig)
 
         def regroup(dst, src):
             nc.vector.tensor_copy(
@@ -100,11 +106,9 @@ def tile_ensembleenvprob_pa_t_kernel(
                 in_=src.rearrange("p t (c i) -> p c t i", i=4),
             )
 
-        wgrp = {}
-
         def wh_regroup(e):
             wgrp[e] = work.tile([P, 4 * HID], BF16, name="whgrp", tag="ggrp", align_bytes=64)
-            regroup(wgrp[e][:], wh_raw[:, e])
+            regroup(wgrp[e][:], wh_raw[e][:])
 
         def wh_quant(e):
             nc.vector.quantize_mx(
@@ -116,7 +120,7 @@ def tile_ensembleenvprob_pa_t_kernel(
             for m in range(2):
                 regroup(
                     wgrp[E + e][:, m * 4 * OD : (m + 1) * 4 * OD],
-                    w2_raw[:, m, 4 * e : 4 * e + 4, :],
+                    w2_raw[m][:, 4 * e : 4 * e + 4, :],
                 )
 
         def w2_quant(e):
@@ -124,30 +128,35 @@ def tile_ensembleenvprob_pa_t_kernel(
                 out=w2q[:, e, :].bitcast(FP8X4), scales=w2s[:, e, :], in_=wgrp[E + e][:]
             )
 
-        xt, hgrp, hq, hs, m1, gpl, ggrp, gq, gs, sg = {}, {}, {}, {}, {}, {}, {}, {}, {}, {}
+        def small_vectors_pe():
+            pv = psum.tile([P, P], BF16, name="pv", tag="b7")
+            nc.tensor.transpose(pv[:], vecs[:], ident_b[:])
+            return pv
 
-        def transposes(i):
-            c, e = divmod(i, E)
-            words = h_tiles[c][:].bitcast(F32)
-            xt[i] = []
-            for half in range(2):
-                x = psum.tile([P, 2, 2 * P], F32, name="x", tag="b%d" % (2 * (i % 2) + half))
-                for tt in range(2):
-                    base = ((2 * half + tt) * E + e) * (HID // 2)
-                    for u in range(2):
-                        nc.tensor.transpose(
-                            x[:, u, tt * P : (tt + 1) * P],
-                            words[:, base + u * P : base + (u + 1) * P],
-                            ident_f[:],
-                        )
-                xt[i].append(x)
+        def small_vectors(pv):
+            nc.vector.tensor_copy(out=cols[:], in_=pv[:, 0:19])
+            nc.vector.tensor_tensor(out=hl[:], in0=cols[:, 15:17], in1=cols[:, 17:19], op=ALU.add)
+            nc.scalar.activation(out=ab[:], in_=hl[:], func=ACT.Exp)
+
+        def transposes(i, half):
+            words = h_tiles[i][:].bitcast(F32)
+            x = psum.tile([P, 2, 2 * P], F32, name="x", tag="b%d" % (2 * (i % 2) + half))
+            for tt in range(2):
+                base = (2 * half + tt) * (HID // 2)
+                for u in range(2):
+                    nc.tensor.transpose(
+                        x[:, u, tt * P : (tt + 1) * P],
+                        words[:, base + u * P : base + (u + 1) * P],
+                        ident_f[:],
+                    )
+            xt[(i, half)] = x
 
         def exits(i):
             hgrp[i] = work.tile([P, 2 * HID], F32, name="hgrp", tag="hgrp", align_bytes=64)
             for half in range(2):
                 dst = hgrp[i][:, half * HID : (half + 1) * HID].rearrange("p (n u) -> p n u", u=2)
-                src = xt[i][half][:].rearrange("p u n -> p n u")
-                if half == 0:
+                src = xt[(i, half)][:].rearrange("p u n -> p n u")
+                if half == 0 or i % SCALAR_TAKES_BOTH == 2:
                     nc.scalar.copy(out=dst, in_=src)
                 else:
                     nc.vector.tensor_copy(out=dst, in_=src)
@@ -160,7 +169,7 @@ def tile_ensembleenvprob_pa_t_kernel(
             )
 
         def stage1(i):
-            e = i % E
+            e = ce(i)[1]
             m1[i] = []
             for j in range(4):
                 acc = psum.tile([P, HID], F32, name="acc", tag="b%d" % (4 + j))
@@ -176,7 +185,7 @@ def tile_ensembleenvprob_pa_t_kernel(
                 m1[i].append(acc)
 
         def silu(i):
-            e = i % E
+            e = ce(i)[1]
             gpl[i] = work.tile([P, 4, HID], BF16, name="gpl", tag="gpl")
             for j in range(4):
                 nc.scalar.activation(
@@ -189,51 +198,95 @@ def tile_ensembleenvprob_pa_t_kernel(
             regroup(ggrp[i][:], gpl[i][:])
 
         def quant_g(i):
-            gq[i] = keep.tile([P, HID], U32, name="gq%d" % i, align_bytes=64)
-            gs[i] = keep.tile([P, HID], U8, name="gs%d" % i, align_bytes=64)
-            nc.vector.quantize_mx(out=gq[i][:].bitcast(FP8X4), scales=gs[i][:], in_=ggrp[i][:])
+            gq[ce(i)] = keep.tile([P, HID], U32, name="gq%d" % i, align_bytes=64)
+            gs[ce(i)] = keep.tile([P, HID], U8, name="gs%d" % i, align_bytes=64)
+            nc.vector.quantize_mx(
+                out=gq[ce(i)][:].bitcast(FP8X4), scales=gs[ce(i)][:], in_=ggrp[i][:]
+            )
 
+        def lookahead(i):
+            transposes(i, 0)
+            transposes(i, 1)
+
+        def after_transposes(i):
+            if i + 7 < NIT:
+                load_h(i + 7)
+
+        load_wh(0)
+        load_h(0, pieces=2)
+        load_h(1)
+        load_h(2)
+        load_wh(1)
+        load_h(3)
+        load_h(4)
+        load_wh(2)
+        load_h(5)
         wh_regroup(0)
-        for tick in range(-2, NIT + 2):
-            if tick >= 0 and tick % E == 0 and tick // E + 2 < CH:
-                c = tick // E + 2
-                h_tiles[c] = big.tile([P, SL * E * HID], BF16, name="h_sb", tag="big")
-                nc.sync.dma_start(out=h_tiles[c][:], in_=h_rows[c])
-            if tick + 2 < NIT:
-                transposes(tick + 2)
-            if 0 <= tick - 1 < NIT:
-                regroup_g(tick - 1)
-            if 0 <= tick < NIT:
-                silu(tick)
-            if 0 <= tick + 1 < NIT:
+        load_h(6)
+        transposes(0, 0)
+        pv = small_vectors_pe()
+        transposes(0, 1)
+        after_transposes(0)
+        small_vectors(pv)
+        wh_quant(0)
+        exits(0)
+        quant_h(0)
+        stage1(0)
+        lookahead(1)
+        after_transposes(1)
+        exits(1)
+        done = 2
+        for tick in range(NIT + 2):
+            new = list(range(done, min(tick + 3, NIT - 1) + 1))
+            done += len(new)
+            if new:
+                lookahead(new[0])
+                after_transposes(new[0])
+            if tick + 1 < NIT:
                 quant_h(tick + 1)
+            if tick < NIT:
+                silu(tick)
+            if tick + 1 < NIT:
                 stage1(tick + 1)
             if 0 <= tick - 1 < NIT:
+                regroup_g(tick - 1)
+            if tick in (2, 5):
+                wh_regroup(1 + (tick - 2) // 3)
+            if tick == 7:
+                load_w2()
+            if tick in (10, 11, 12):
+                w2_regroup(tick - 10)
+            if new:
+                exits(new[0])
+            for i in new[1:]:
+                lookahead(i)
+                after_transposes(i)
+                exits(i)
+            if 0 <= tick - 1 < NIT:
                 quant_g(tick - 1)
-            if tick == -2:
-                wh_quant(0)
-            if tick in (-1, 0):
-                wh_quant(tick + 2)
-            if tick in (1, 2, 3):
-                w2_quant(tick - 1)
-            if tick + 2 < NIT:
-                exits(tick + 2)
-            if tick in (-2, -1):
-                wh_regroup(tick + 3)
-            if tick in (0, 1, 2):
-                w2_regroup(tick)
-            if tick == 3:
+            if tick in (3, 6):
+                wh_quant(1 + (tick - 3) // 3)
+            if tick in (11, 12, 13):
+                w2_quant(tick - 11)
+            if tick == 14:
                 nc.vector.tensor_copy(out=bmu_f[:], in_=bmu_b[:])
+            if tick == 21:
+                pv2 = psum.tile([P, P], BF16, name="pv2", tag="b0")
+                nc.tensor.transpose(pv2[:], vecs2[:], ident_b[:])
+                nc.vector.tensor_copy(out=cols2[:], in_=pv2[:, 0:E])
+                nc.vector.tensor_scalar(
+                    out=c2[:], in0=cols2[:], scalar1=2.0, scalar2=hl[:, 0:1],
+                    op0=ALU.mult, op1=ALU.subtract,
+                )
 
-        ds = {}
         for i in range(NIT):
             c, e = divmod(i, E)
             pm = psum.tile([P, SL, OD], F32, name="pm", tag="b%d" % (i % 4))
             for t in range(SL):
                 nc.tensor.matmul_mx(
                     out=pm[:, t, :],
-                    lhsT=gq[i][:, t * P : (t + 1) * P].bitcast(FP8X4),
-                    lhsT_scale=gs[i][:, t * P : (t + 1) * P],
+                    lhsT=gq[(c, e)][:, t * P : (t + 1) * P].bitcast(FP8X4),
+                    lhsT_scale=gs[(c, e)][:, t * P : (t + 1) * P],
                     rhs=w2q[:, e, 0:OD].bitcast(FP8X4),
                     rhs_scale=w2s[:, e, 0:OD],
                     start=True,
@@ -244,8 +297,8 @@ def tile_ensembleenvprob_pa_t_kernel(
                 out=pg[:],
                 lhsT=w2q[:, e, OD : 2 * OD].bitcast(FP8X4),
                 lhsT_scale=w2s[:, e, OD : 2 * OD],
-                rhs=gq[i][:].bitcast(FP8X4),
-                rhs_scale=gs[i][:],
+                rhs=gq[(c, e)][:].bitcast(FP8X4),
+                rhs_scale=gs[(c, e)][:],
                 start=True,
                 stop=True,
             )
@@ -254,9 +307,9 @@ def tile_ensembleenvprob_pa_t_kernel(
                 out=sg[i][:], in_=pg[:], func=ACT.Sigmoid, bias=c2[:, e : e + 1], scale=2.0
             )
             if e == 0:
-                ds[c] = big.tile([P, SL, E, SD], F32, name="ds_mu", tag="big")
+                ds[c] = io.tile([P, SL, E * SD], F32, name="ds_mu", tag="io")
             nc.vector.tensor_tensor(
-                out=ds[c][:, :, e, :], in0=pm[:, :, 0:SD],
+                out=ds[c][:, :, e * SD : (e + 1) * SD], in0=pm[:, :, 0:SD],
                 in1=bmu_f[:, e * OD : e * OD + SD].unsqueeze(1).to_broadcast([P, SL, SD]),
                 op=ALU.add,
             )
@@ -266,9 +319,10 @@ def tile_ensembleenvprob_pa_t_kernel(
                 op=ALU.add,
             )
             if e == E - 1:
-                nc.sync.dma_start(out=ds_mu_rows[c], in_=ds[c][:].rearrange("p t e o -> p (t e o)"))
-        nc.sync.dma_start(out=r_mu_rows, in_=r_mu[:].rearrange("p c t e o -> p (c t e o)"))
+                nc.sync.dma_start(out=ds_mu_rows[c], in_=ds[c][:])
+        nc.sync.dma_start(out=r_mu_rows, in_=r_mu[:].rearrange("p c t e o -> p c (t e o)"))
 
+        r_sg_view = r_sg[:].rearrange("p c t e o -> p c (t e o)")
         for i in range(NIT):
             c, e = divmod(i, E)
             nc.scalar.activation(
@@ -278,9 +332,19 @@ def tile_ensembleenvprob_pa_t_kernel(
             for t in range(SL):
                 nc.tensor.transpose(pt[:, t, :], sg[i][:, t * P : (t + 1) * P], ident_f[:])
             if e == 0:
-                ds[c] = big.tile([P, SL, E, SD], F32, name="ds_sg", tag="big")
-            nc.vector.tensor_copy(out=ds[c][:, :, e, :], in_=pt[:, :, 0:SD])
+                ds[c] = io.tile([P, SL, E * SD], F32, name="ds_sg", tag="io")
+            nc.vector.tensor_copy(out=ds[c][:, :, e * SD : (e + 1) * SD], in_=pt[:, :, 0:SD])
             nc.vector.tensor_copy(out=r_sg[:, c, :, e, :], in_=pt[:, :, SD:OD])
-            if e == E - 1:
-                nc.sync.dma_start(out=ds_sg_rows[c], in_=ds[c][:].rearrange("p t e o -> p (t e o)"))
-        nc.sync.dma_start(out=r_sg_rows, in_=r_sg[:].rearrange("p c t e o -> p (c t e o)"))
+            if c < CH - 1 and e == E - 1:
+                nc.sync.dma_start(out=ds_sg_rows[c], in_=ds[c][:])
+            if c == CH - 2 and e == E - 1:
+                nc.sync.dma_start(out=r_sg_rows[:, 0 : CH - 1], in_=r_sg_view[:, 0 : CH - 1])
+            if c == CH - 1 and e == E - 2:
+                nc.sync.dma_start(
+                    out=ds_sg_rows[c][:, :, 0 : 2 * SD], in_=ds[c][:, :, 0 : 2 * SD]
+                )
+            if c == CH - 1 and e == E - 1:
+                nc.sync.dma_start(
+                    out=ds_sg_rows[c][:, :, 2 * SD : 3 * SD], in_=ds[c][:, :, 2 * SD : 3 * SD]
+                )
+        nc.sync.dma_start(out=r_sg_rows[:, CH - 1 : CH], in_=r_sg_view[:, CH - 1 : CH])

@@ -18,7 +18,8 @@ SL = 4
 NIT = CH * E
 FLOPS = 2 * N * E * HID * (HID + 2 * OD)
 MANUAL = True
-SCALAR_TAKES_BOTH = 5
+X_ENGINES = {0: "VV", 1: "VV", 2: "VV", 4: "SS", 6: "SS", 7: "SS", 8: "SS"}
+SCALAR_SIGMA_OUT = (18, 21)
 
 
 def tile_ensembleenvprob_pa_t_kernel(
@@ -93,10 +94,12 @@ def tile_ensembleenvprob_pa_t_kernel(
                 in_=Wh[e].rearrange("(u p a) f -> p u (a f)", u=2, a=2),
             )
 
-        def load_w2():
-            for m, w in enumerate((Wmu, Wsig)):
-                w2_raw[m] = io.tile([P, E * 4, OD], BF16, name="w2_raw", tag="io")
-                nc.sync.dma_start(out=w2_raw[m][:], in_=w.rearrange("e (j p) o -> p (e j) o", p=P))
+        def load_w2(m):
+            w2_raw[m] = io.tile([P, E * 4, OD], BF16, name="w2_raw", tag="io")
+            w = (Wmu, Wsig)[m]
+            nc.sync.dma_start(out=w2_raw[m][:], in_=w.rearrange("e (j p) o -> p (e j) o", p=P))
+
+        def load_late_vectors():
             nc.sync.dma_start(out=bmu_b[:], in_=bmu.rearrange("e o -> (e o)").partition_broadcast(P))
             nc.sync.dma_start(out=vecs2[0:E, :], in_=bsig)
 
@@ -156,7 +159,7 @@ def tile_ensembleenvprob_pa_t_kernel(
             for half in range(2):
                 dst = hgrp[i][:, half * HID : (half + 1) * HID].rearrange("p (n u) -> p n u", u=2)
                 src = xt[(i, half)][:].rearrange("p u n -> p n u")
-                if half == 0 or i % SCALAR_TAKES_BOTH == 2:
+                if X_ENGINES.get(i, "SV")[half] == "S":
                     nc.scalar.copy(out=dst, in_=src)
                 else:
                     nc.vector.tensor_copy(out=dst, in_=src)
@@ -204,44 +207,54 @@ def tile_ensembleenvprob_pa_t_kernel(
                 out=gq[ce(i)][:].bitcast(FP8X4), scales=gs[ce(i)][:], in_=ggrp[i][:]
             )
 
-        def lookahead(i):
-            transposes(i, 0)
-            transposes(i, 1)
+        load_list = [("wh", 0), ("h", 0), ("h", 1), ("wh", 1), ("h", 2), ("wh", 2), ("h", 3), ("w2", 0), ("h", 4), ("w2", 1)]
+        load_list.extend([("h", i) for i in range(5, NIT)])
+        issued = [0]
 
-        def after_transposes(i):
-            if i + 7 < NIT:
-                load_h(i + 7)
+        def loads(n):
+            for unused in range(n):
+                if issued[0] < len(load_list):
+                    kind, k = load_list[issued[0]]
+                    issued[0] += 1
+                    if kind == "wh":
+                        load_wh(k)
+                    elif kind == "w2":
+                        load_w2(k)
+                    else:
+                        load_h(k, pieces=2 if k == 0 else 1)
 
-        load_wh(0)
-        load_h(0, pieces=2)
-        load_h(1)
-        load_h(2)
-        load_wh(1)
-        load_h(3)
-        load_h(4)
-        load_wh(2)
-        load_h(5)
+        hooks = {
+            0: [(wh_regroup, 1)],
+            1: [(wh_quant, 1)],
+            2: [(wh_regroup, 2)],
+            3: [(wh_quant, 2)],
+            4: [(w2_regroup, 0)],
+            5: [(w2_quant, 0), (w2_regroup, 1)],
+            6: [(w2_quant, 1), (w2_regroup, 2)],
+            7: [(w2_quant, 2)],
+        }
+
+        loads(8)
         wh_regroup(0)
-        load_h(6)
         transposes(0, 0)
         pv = small_vectors_pe()
         transposes(0, 1)
-        after_transposes(0)
         small_vectors(pv)
         wh_quant(0)
         exits(0)
+        loads(1)
+        transposes(1, 0)
+        transposes(1, 1)
         quant_h(0)
         stage1(0)
-        lookahead(1)
-        after_transposes(1)
+        loads(1)
         exits(1)
-        done = 2
         for tick in range(NIT + 2):
-            new = list(range(done, min(tick + 3, NIT - 1) + 1))
-            done += len(new)
-            if new:
-                lookahead(new[0])
-                after_transposes(new[0])
+            ahead = tick + 2
+            if ahead < NIT:
+                transposes(ahead, 0)
+                transposes(ahead, 1)
+                loads(1)
             if tick + 1 < NIT:
                 quant_h(tick + 1)
             if tick < NIT:
@@ -250,27 +263,17 @@ def tile_ensembleenvprob_pa_t_kernel(
                 stage1(tick + 1)
             if 0 <= tick - 1 < NIT:
                 regroup_g(tick - 1)
-            if tick in (2, 5):
-                wh_regroup(1 + (tick - 2) // 3)
-            if tick == 7:
-                load_w2()
-            if tick in (10, 11, 12):
-                w2_regroup(tick - 10)
-            if new:
-                exits(new[0])
-            for i in new[1:]:
-                lookahead(i)
-                after_transposes(i)
-                exits(i)
+            if ahead < NIT:
+                exits(ahead)
+            for fn, arg in hooks.get(tick, []):
+                fn(arg)
+            if tick == 8:
+                load_late_vectors()
+            if tick == 12:
+                nc.vector.tensor_copy(out=bmu_f[:], in_=bmu_b[:])
             if 0 <= tick - 1 < NIT:
                 quant_g(tick - 1)
-            if tick in (3, 6):
-                wh_quant(1 + (tick - 3) // 3)
-            if tick in (11, 12, 13):
-                w2_quant(tick - 11)
-            if tick == 14:
-                nc.vector.tensor_copy(out=bmu_f[:], in_=bmu_b[:])
-            if tick == 21:
+            if tick == 22:
                 pv2 = psum.tile([P, P], BF16, name="pv2", tag="b0")
                 nc.tensor.transpose(pv2[:], vecs2[:], ident_b[:])
                 nc.vector.tensor_copy(out=cols2[:], in_=pv2[:, 0:E])
@@ -279,19 +282,8 @@ def tile_ensembleenvprob_pa_t_kernel(
                     op0=ALU.mult, op1=ALU.subtract,
                 )
 
-        for i in range(NIT):
+        def sigma_head(i):
             c, e = divmod(i, E)
-            pm = psum.tile([P, SL, OD], F32, name="pm", tag="b%d" % (i % 4))
-            for t in range(SL):
-                nc.tensor.matmul_mx(
-                    out=pm[:, t, :],
-                    lhsT=gq[(c, e)][:, t * P : (t + 1) * P].bitcast(FP8X4),
-                    lhsT_scale=gs[(c, e)][:, t * P : (t + 1) * P],
-                    rhs=w2q[:, e, 0:OD].bitcast(FP8X4),
-                    rhs_scale=w2s[:, e, 0:OD],
-                    start=True,
-                    stop=True,
-                )
             pg = psum.tile([P, HID], F32, name="pg", tag="b%d" % (4 + i % 4))
             nc.tensor.matmul_mx(
                 out=pg[:],
@@ -306,6 +298,20 @@ def tile_ensembleenvprob_pa_t_kernel(
             nc.scalar.activation(
                 out=sg[i][:], in_=pg[:], func=ACT.Sigmoid, bias=c2[:, e : e + 1], scale=2.0
             )
+
+        def mu_head(i):
+            c, e = divmod(i, E)
+            pm = psum.tile([P, SL, OD], F32, name="pm", tag="b%d" % (i % 4))
+            for t in range(SL):
+                nc.tensor.matmul_mx(
+                    out=pm[:, t, :],
+                    lhsT=gq[(c, e)][:, t * P : (t + 1) * P].bitcast(FP8X4),
+                    lhsT_scale=gs[(c, e)][:, t * P : (t + 1) * P],
+                    rhs=w2q[:, e, 0:OD].bitcast(FP8X4),
+                    rhs_scale=w2s[:, e, 0:OD],
+                    start=True,
+                    stop=True,
+                )
             if e == 0:
                 ds[c] = io.tile([P, SL, E * SD], F32, name="ds_mu", tag="io")
             nc.vector.tensor_tensor(
@@ -320,31 +326,48 @@ def tile_ensembleenvprob_pa_t_kernel(
             )
             if e == E - 1:
                 nc.sync.dma_start(out=ds_mu_rows[c], in_=ds[c][:])
+
+        for i in range(NIT + 1):
+            if i < NIT:
+                sigma_head(i)
+            if i >= 1:
+                mu_head(i - 1)
         nc.sync.dma_start(out=r_mu_rows, in_=r_mu[:].rearrange("p c t e o -> p c (t e o)"))
 
         r_sg_view = r_sg[:].rearrange("p c t e o -> p c (t e o)")
-        for i in range(NIT):
-            c, e = divmod(i, E)
+        pt = {}
+
+        def sqrt_and_back(i):
             nc.scalar.activation(
                 out=sg[i][:], in_=sg[i][:], func=ACT.Sqrt, bias=ab[:, 1:2], scale=ab[:, 0:1]
             )
-            pt = psum.tile([P, SL, OD], F32, name="pt", tag="b%d" % (i % 8))
+            pt[i] = psum.tile([P, SL, OD], F32, name="pt", tag="b%d" % (i % 8))
             for t in range(SL):
-                nc.tensor.transpose(pt[:, t, :], sg[i][:, t * P : (t + 1) * P], ident_f[:])
+                nc.tensor.transpose(pt[i][:, t, :], sg[i][:, t * P : (t + 1) * P], ident_f[:])
+
+        def sigma_out(i):
+            c, e = divmod(i, E)
+            last = c == CH - 1
             if e == 0:
-                ds[c] = io.tile([P, SL, E * SD], F32, name="ds_sg", tag="io")
-            nc.vector.tensor_copy(out=ds[c][:, :, e * SD : (e + 1) * SD], in_=pt[:, :, 0:SD])
-            nc.vector.tensor_copy(out=r_sg[:, c, :, e, :], in_=pt[:, :, SD:OD])
-            if c < CH - 1 and e == E - 1:
+                ds[c] = io.tile([P, SL, (2 if last else E) * SD], F32, name="ds_sg", tag="io")
+            if last and e == E - 1:
+                ds[c] = io.tile([P, SL, SD], F32, name="ds_sg_end", tag="io")
+            col = 0 if (last and e == E - 1) else e * SD
+            copy = nc.scalar.copy if i in SCALAR_SIGMA_OUT else nc.vector.tensor_copy
+            copy(out=ds[c][:, :, col : col + SD], in_=pt[i][:, :, 0:SD])
+            copy(out=r_sg[:, c, :, e, :], in_=pt[i][:, :, SD:OD])
+            if not last and e == E - 1:
                 nc.sync.dma_start(out=ds_sg_rows[c], in_=ds[c][:])
             if c == CH - 2 and e == E - 1:
                 nc.sync.dma_start(out=r_sg_rows[:, 0 : CH - 1], in_=r_sg_view[:, 0 : CH - 1])
-            if c == CH - 1 and e == E - 2:
-                nc.sync.dma_start(
-                    out=ds_sg_rows[c][:, :, 0 : 2 * SD], in_=ds[c][:, :, 0 : 2 * SD]
-                )
-            if c == CH - 1 and e == E - 1:
-                nc.sync.dma_start(
-                    out=ds_sg_rows[c][:, :, 2 * SD : 3 * SD], in_=ds[c][:, :, 2 * SD : 3 * SD]
-                )
+            if last and e == E - 2:
+                nc.sync.dma_start(out=ds_sg_rows[c][:, :, 0 : 2 * SD], in_=ds[c][:])
+            if last and e == E - 1:
+                nc.sync.dma_start(out=ds_sg_rows[c][:, :, 2 * SD : 3 * SD], in_=ds[c][:])
+
+        for i in range(NIT + 2):
+            if i < NIT:
+                sqrt_and_back(i)
+            if i >= 2:
+                sigma_out(i - 2)
         nc.sync.dma_start(out=r_sg_rows[:, CH - 1 : CH], in_=r_sg_view[:, CH - 1 : CH])

@@ -12,14 +12,18 @@ ACT = mybir.ActivationFunctionType
 ALU = mybir.AluOpType
 
 N, E, HID, OD, SD = 4096, 3, 512, 128, 120
+RD = OD - SD
 P = 128
+PACK = 4
 CH = 8
-SL = 4
+SL = N // (CH * P)
+COLS = SL * P
 NIT = CH * E
+AHEAD = 2
+IO_SLOTS = 9
+VECTOR_ONLY = 3
+SCALAR_ONLY = 7
 FLOPS = 2 * N * E * HID * (HID + 2 * OD)
-MANUAL = True
-X_ENGINES = {0: "VV", 1: "VV", 2: "VV", 4: "SS", 6: "SS", 7: "SS", 8: "SS"}
-SCALAR_SIGMA_OUT = (18, 21)
 
 
 def tile_ensembleenvprob_pa_t_kernel(
@@ -30,344 +34,317 @@ def tile_ensembleenvprob_pa_t_kernel(
     with ExitStack() as ctx:
         const = ctx.enter_context(tc.tile_pool(name="const", bufs=1))
         keep = ctx.enter_context(tc.tile_pool(name="keep", bufs=1))
-        io = ctx.enter_context(tc.tile_pool(name="io", bufs=9))
+        io = ctx.enter_context(tc.tile_pool(name="io", bufs=IO_SLOTS))
         work = ctx.enter_context(tc.tile_pool(name="work", bufs=3))
         psum = ctx.enter_context(tc.psum_pool(name="psum", bufs=1))
-        if MANUAL:
-            ctx.enter_context(tc.manual_schedule())
+        ctx.enter_context(tc.manual_schedule())
 
-        h_by_e = h.rearrange("(p c t) e k -> c e p t k", c=CH, t=SL)
-        ds_mu_rows = out_0.rearrange("(p c t) e o -> c p t (e o)", c=CH, t=SL)
-        ds_sg_rows = out_1.rearrange("(p c t) e o -> c p t (e o)", c=CH, t=SL)
-        r_mu_rows = out_2.rearrange("(p c t) e o -> p c (t e o)", c=CH, t=SL)
-        r_sg_rows = out_3.rearrange("(p c t) e o -> p c (t e o)", c=CH, t=SL)
+        h_view = h.rearrange("(p c t) e k -> c e p t k", c=CH, t=SL)
+        ds_mu_view = out_0.rearrange("(p c t) e o -> c p t (e o)", c=CH, t=SL)
+        ds_sg_view = out_1.rearrange("(p c t) e o -> c p t (e o)", c=CH, t=SL)
+        r_mu_view = out_2.rearrange("(p c t) e o -> c p (t e o)", c=CH, t=SL)
+        r_sg_view = out_3.rearrange("(p c t) e o -> c p (t e o)", c=CH, t=SL)
+
+        def bank(k, shape, dtype=F32):
+            return psum.tile(shape, dtype, name="bank", tag="bank%d" % k)
 
         ident_f = const.tile([P, P], F32, name="ident_f")
         make_identity(nc, ident_f[:])
         ident_b = const.tile([P, P], BF16, name="ident_b")
         make_identity(nc, ident_b[:])
-        vecs = const.tile([P, P], BF16, name="vecs")
-        nc.vector.memset(vecs[:], 0.0)
-        nc.scalar.dma_start(out=vecs[0:12, :], in_=bh.rearrange("e (j p) -> (e j) p", p=P))
-        nc.scalar.dma_start(out=vecs[15:16, 0:SD], in_=max_lv_s)
-        nc.scalar.dma_start(out=vecs[16:17, 0:SD], in_=min_lv_s)
-        nc.scalar.dma_start(out=vecs[17:18, SD:OD], in_=max_lv_r)
-        nc.scalar.dma_start(out=vecs[18:19, SD:OD], in_=min_lv_r)
-        vecs2 = const.tile([P, P], BF16, name="vecs2")
-        nc.vector.memset(vecs2[:], 0.0)
+        early = const.tile([P, P], BF16, name="early")
+        nc.vector.memset(early[:], 0.0)
+        late = const.tile([P, P], BF16, name="late")
+        nc.vector.memset(late[:], 0.0)
+        nc.scalar.dma_start(out=early[0 : E * PACK, :], in_=bh.rearrange("e (j p) -> (e j) p", p=P))
+        nc.scalar.dma_start(out=early[12:13, 0:SD], in_=max_lv_s)
+        nc.scalar.dma_start(out=early[13:14, 0:SD], in_=min_lv_s)
+        nc.scalar.dma_start(out=early[14:15, SD:OD], in_=max_lv_r)
+        nc.scalar.dma_start(out=early[15:16, SD:OD], in_=min_lv_r)
 
-        whq = const.tile([P, E, HID], U32, name="whq", align_bytes=64)
-        whs = const.tile([P, E, HID], U8, name="whs", align_bytes=64)
-        w2q = const.tile([P, E, 2 * OD], U32, name="w2q", align_bytes=64)
-        w2s = const.tile([P, E, 2 * OD], U8, name="w2s", align_bytes=64)
-        r_mu = const.tile([P, CH, SL, E, OD - SD], F32, name="r_mu")
-        r_sg = const.tile([P, CH, SL, E, OD - SD], F32, name="r_sg")
-        bmu_b = const.tile([P, E * OD], BF16, name="bmu_b")
-        bmu_f = const.tile([P, E * OD], F32, name="bmu_f")
-        cols = const.tile([P, 19], F32, name="cols")
-        cols2 = const.tile([P, E], F32, name="cols2")
-        hl = const.tile([P, 2], F32, name="hl")
-        c2 = const.tile([P, E], F32, name="c2")
-        ab = const.tile([P, 2], F32, name="ab")
+        wh_codes = const.tile([P, E, HID], U32, name="wh_codes", align_bytes=64)
+        wh_scales = const.tile([P, E, HID], U8, name="wh_scales", align_bytes=64)
+        head_codes = const.tile([P, E, 2 * OD], U32, name="head_codes", align_bytes=64)
+        head_scales = const.tile([P, E, 2 * OD], U8, name="head_scales", align_bytes=64)
+        bmu_bf = const.tile([P, E * OD], BF16, name="bmu_bf")
+        bmu_all = const.tile([P, E * OD], F32, name="bmu_all")
+        early_cols = const.tile([P, 16], F32, name="early_cols")
+        late_cols = const.tile([P, E], F32, name="late_cols")
+        hi_lo = const.tile([P, 2], F32, name="hi_lo")
+        exp_hi_lo = const.tile([P, 2], F32, name="exp_hi_lo")
+        sig_bias = const.tile([P, E], F32, name="sig_bias")
 
-        h_tiles, wh_raw, w2_raw, wgrp = {}, {}, {}, {}
-        xt, hgrp, hq, hs, m1, gpl, ggrp, gq, gs, sg, ds = {}, {}, {}, {}, {}, {}, {}, {}, {}, {}, {}
+        h_sb, w_raw, w_grouped = {}, {}, {}
+        xt, h_grouped, h_codes, h_scales, acc, g_planes, g_grouped = {}, {}, {}, {}, {}, {}, {}
+        g_codes, g_scales, sg, back, ds, rw = {}, {}, {}, {}, {}, {}
 
-        def ce(i):
-            return i % CH, i // CH
+        def member_chunk(i):
+            return i // CH, i % CH
 
-        def load_h(i, pieces=1):
-            c, e = ce(i)
-            h_tiles[i] = io.tile([P, SL * HID], BF16, name="h_sb", tag="io")
-            view = h_tiles[i][:].rearrange("p (t k) -> p t k", t=SL)
+        def load_h(i):
+            e, c = member_chunk(i)
+            h_sb[i] = io.tile([P, SL, HID], BF16, name="h_sb", tag="io")
+            pieces = 2 if i == 0 else 1
             step = SL // pieces
             for s in range(pieces):
+                rows = slice(s * step, (s + 1) * step)
+                nc.sync.dma_start(out=h_sb[i][:, rows, :], in_=h_view[c, e][:, rows, :])
+
+        def load_weights(w):
+            if w < E:
+                w_raw[w] = io.tile([P, PACK, HID], BF16, name="w_raw", tag="io")
                 nc.sync.dma_start(
-                    out=view[:, s * step : (s + 1) * step, :],
-                    in_=h_by_e[c, e][:, s * step : (s + 1) * step, :],
+                    out=w_raw[w][:].rearrange("p (u a) f -> p u (a f)", u=2),
+                    in_=Wh[w].rearrange("(u p a) f -> p u (a f)", u=2, a=2),
                 )
+            else:
+                w_raw[w] = io.tile([P, PACK, 2 * OD], BF16, name="w_raw", tag="io")
+                for m, head in enumerate((Wmu, Wsig)):
+                    nc.sync.dma_start(
+                        out=w_raw[w][:, :, m * OD : (m + 1) * OD],
+                        in_=head[w - E].rearrange("(j p) o -> p j o", p=P),
+                    )
 
-        def load_wh(e):
-            wh_raw[e] = io.tile([P, 4, HID], BF16, name="wh_raw", tag="io")
-            nc.sync.dma_start(
-                out=wh_raw[e][:].rearrange("p (u a) f -> p u (a f)", u=2),
-                in_=Wh[e].rearrange("(u p a) f -> p u (a f)", u=2, a=2),
-            )
+        load_order = [("w", 0), ("h", 0)]
+        for i in range(1, NIT):
+            load_order.append(("h", i))
+            if i < 2 * E:
+                load_order.append(("w", i))
+        issued = [0]
 
-        def load_w2(m):
-            w2_raw[m] = io.tile([P, E * 4, OD], BF16, name="w2_raw", tag="io")
-            w = (Wmu, Wsig)[m]
-            nc.sync.dma_start(out=w2_raw[m][:], in_=w.rearrange("e (j p) o -> p (e j) o", p=P))
-
-        def load_late_vectors():
-            nc.sync.dma_start(out=bmu_b[:], in_=bmu.rearrange("e o -> (e o)").partition_broadcast(P))
-            nc.sync.dma_start(out=vecs2[0:E, :], in_=bsig)
+        def next_loads(count):
+            for kind, k in load_order[issued[0] : issued[0] + count]:
+                if kind == "w":
+                    load_weights(k)
+                else:
+                    load_h(k)
+            issued[0] += count
 
         def regroup(dst, src):
             nc.vector.tensor_copy(
-                out=dst.rearrange("p (c i t) -> p c t i", i=4, t=4),
+                out=dst.rearrange("p (c i t) -> p c t i", i=4, t=PACK),
                 in_=src.rearrange("p t (c i) -> p c t i", i=4),
             )
 
-        def wh_regroup(e):
-            wgrp[e] = work.tile([P, 4 * HID], BF16, name="whgrp", tag="ggrp", align_bytes=64)
-            regroup(wgrp[e][:], wh_raw[e][:])
+        def regroup_weights(w):
+            width = HID if w < E else 2 * OD
+            w_grouped[w] = work.tile([P, PACK * width], BF16, name="w_grouped", tag="grouped", align_bytes=64)
+            regroup(w_grouped[w][:], w_raw[w][:])
+            next_loads(1)
 
-        def wh_quant(e):
+        def quantise_weights(w):
+            codes, scales = (wh_codes, wh_scales) if w < E else (head_codes, head_scales)
             nc.vector.quantize_mx(
-                out=whq[:, e, :].bitcast(FP8X4), scales=whs[:, e, :], in_=wgrp[e][:]
+                out=codes[:, w % E, :].bitcast(FP8X4), scales=scales[:, w % E, :], in_=w_grouped[w][:]
             )
-
-        def w2_regroup(e):
-            wgrp[E + e] = work.tile([P, 8 * OD], BF16, name="w2grp", tag="ggrp", align_bytes=64)
-            for m in range(2):
-                regroup(
-                    wgrp[E + e][:, m * 4 * OD : (m + 1) * 4 * OD],
-                    w2_raw[m][:, 4 * e : 4 * e + 4, :],
-                )
-
-        def w2_quant(e):
-            nc.vector.quantize_mx(
-                out=w2q[:, e, :].bitcast(FP8X4), scales=w2s[:, e, :], in_=wgrp[E + e][:]
-            )
-
-        def small_vectors_pe():
-            pv = psum.tile([P, P], BF16, name="pv", tag="b7")
-            nc.tensor.transpose(pv[:], vecs[:], ident_b[:])
-            return pv
-
-        def small_vectors(pv):
-            nc.vector.tensor_copy(out=cols[:], in_=pv[:, 0:19])
-            nc.vector.tensor_tensor(out=hl[:], in0=cols[:, 15:17], in1=cols[:, 17:19], op=ALU.add)
-            nc.scalar.activation(out=ab[:], in_=hl[:], func=ACT.Exp)
 
         def transposes(i, half):
-            words = h_tiles[i][:].bitcast(F32)
-            x = psum.tile([P, 2, 2 * P], F32, name="x", tag="b%d" % (2 * (i % 2) + half))
+            words = h_sb[i][:].rearrange("p t k -> p (t k)").bitcast(F32)
+            xt[(i, half)] = bank(2 * (i % 2) + half, [P, 2, 2 * P])
             for tt in range(2):
                 base = (2 * half + tt) * (HID // 2)
                 for u in range(2):
                     nc.tensor.transpose(
-                        x[:, u, tt * P : (tt + 1) * P],
+                        xt[(i, half)][:, u, tt * P : (tt + 1) * P],
                         words[:, base + u * P : base + (u + 1) * P],
                         ident_f[:],
                     )
-            xt[(i, half)] = x
+            if half == 1:
+                next_loads(1)
 
-        def exits(i):
-            hgrp[i] = work.tile([P, 2 * HID], F32, name="hgrp", tag="hgrp", align_bytes=64)
+        def copy_out(i):
             for half in range(2):
-                dst = hgrp[i][:, half * HID : (half + 1) * HID].rearrange("p (n u) -> p n u", u=2)
+                h_grouped[(i, half)] = work.tile(
+                    [P, HID], F32, name="h_grouped", tag="h_grouped%d" % half, align_bytes=64
+                )
+                dst = h_grouped[(i, half)][:].rearrange("p (n u) -> p n u", u=2)
                 src = xt[(i, half)][:].rearrange("p u n -> p n u")
-                if X_ENGINES.get(i, "SV")[half] == "S":
+                on_scalar = (half == 0 and i >= VECTOR_ONLY) or VECTOR_ONLY <= i < SCALAR_ONLY
+                if on_scalar:
                     nc.scalar.copy(out=dst, in_=src)
                 else:
                     nc.vector.tensor_copy(out=dst, in_=src)
 
-        def quant_h(i):
-            hq[i] = work.tile([P, HID], U32, name="hq", tag="hq", align_bytes=64)
-            hs[i] = work.tile([P, HID], U8, name="hs", tag="hs", align_bytes=64)
-            nc.vector.quantize_mx(
-                out=hq[i][:].bitcast(FP8X4), scales=hs[i][:], in_=hgrp[i][:].bitcast(BF16)
-            )
+        def quantise_h(i):
+            h_codes[i] = work.tile([P, COLS], U32, name="h_codes", tag="h_codes", align_bytes=64)
+            h_scales[i] = work.tile([P, COLS], U8, name="h_scales", tag="h_scales", align_bytes=64)
+            for half in range(2):
+                cols = slice(half * COLS // 2, (half + 1) * COLS // 2)
+                nc.vector.quantize_mx(
+                    out=h_codes[i][:, cols].bitcast(FP8X4),
+                    scales=h_scales[i][:, cols],
+                    in_=h_grouped[(i, half)][:].bitcast(BF16),
+                )
 
-        def stage1(i):
-            e = ce(i)[1]
-            m1[i] = []
-            for j in range(4):
-                acc = psum.tile([P, HID], F32, name="acc", tag="b%d" % (4 + j))
+        def layer(i):
+            e = member_chunk(i)[0]
+            for j in range(PACK):
+                acc[(i, j)] = bank(4 + j, [P, COLS])
                 nc.tensor.matmul_mx(
-                    out=acc[:],
-                    lhsT=whq[:, e, j * P : (j + 1) * P].bitcast(FP8X4),
-                    lhsT_scale=whs[:, e, j * P : (j + 1) * P],
-                    rhs=hq[i][:].bitcast(FP8X4),
-                    rhs_scale=hs[i][:],
+                    out=acc[(i, j)][:],
+                    lhsT=wh_codes[:, e, j * P : (j + 1) * P].bitcast(FP8X4),
+                    lhsT_scale=wh_scales[:, e, j * P : (j + 1) * P],
+                    rhs=h_codes[i][:].bitcast(FP8X4),
+                    rhs_scale=h_scales[i][:],
                     start=True,
                     stop=True,
                 )
-                m1[i].append(acc)
 
-        def silu(i):
-            e = ce(i)[1]
-            gpl[i] = work.tile([P, 4, HID], BF16, name="gpl", tag="gpl")
-            for j in range(4):
+        def swish(i):
+            e = member_chunk(i)[0]
+            g_planes[i] = work.tile([P, PACK, COLS], BF16, name="g_planes", tag="g_planes")
+            for j in range(PACK):
                 nc.scalar.activation(
-                    out=gpl[i][:, j, :], in_=m1[i][j][:], func=ACT.Silu,
-                    bias=cols[:, 4 * e + j : 4 * e + j + 1], scale=1.0,
+                    out=g_planes[i][:, j, :], in_=acc[(i, j)][:], func=ACT.Silu,
+                    bias=early_cols[:, PACK * e + j : PACK * e + j + 1], scale=1.0,
                 )
 
         def regroup_g(i):
-            ggrp[i] = work.tile([P, 4 * HID], BF16, name="ggrp", tag="ggrp", align_bytes=64)
-            regroup(ggrp[i][:], gpl[i][:])
+            g_grouped[i] = work.tile([P, PACK * COLS], BF16, name="g_grouped", tag="grouped", align_bytes=64)
+            regroup(g_grouped[i][:], g_planes[i][:])
 
-        def quant_g(i):
-            gq[ce(i)] = keep.tile([P, HID], U32, name="gq%d" % i, align_bytes=64)
-            gs[ce(i)] = keep.tile([P, HID], U8, name="gs%d" % i, align_bytes=64)
+        def quantise_g(i):
+            g_codes[i] = keep.tile([P, COLS], U32, name="g_codes%d" % i, align_bytes=64)
+            g_scales[i] = keep.tile([P, COLS], U8, name="g_scales%d" % i, align_bytes=64)
             nc.vector.quantize_mx(
-                out=gq[ce(i)][:].bitcast(FP8X4), scales=gs[ce(i)][:], in_=ggrp[i][:]
+                out=g_codes[i][:].bitcast(FP8X4), scales=g_scales[i][:], in_=g_grouped[i][:]
             )
 
-        load_list = [("wh", 0), ("h", 0), ("h", 1), ("wh", 1), ("h", 2), ("wh", 2), ("h", 3), ("w2", 0), ("h", 4), ("w2", 1)]
-        load_list.extend([("h", i) for i in range(5, NIT)])
-        issued = [0]
-
-        def loads(n):
-            for unused in range(n):
-                if issued[0] < len(load_list):
-                    kind, k = load_list[issued[0]]
-                    issued[0] += 1
-                    if kind == "wh":
-                        load_wh(k)
-                    elif kind == "w2":
-                        load_w2(k)
-                    else:
-                        load_h(k, pieces=2 if k == 0 else 1)
-
-        hooks = {
-            0: [(wh_regroup, 1)],
-            1: [(wh_quant, 1)],
-            2: [(wh_regroup, 2)],
-            3: [(wh_quant, 2)],
-            4: [(w2_regroup, 0)],
-            5: [(w2_quant, 0), (w2_regroup, 1)],
-            6: [(w2_quant, 1), (w2_regroup, 2)],
-            7: [(w2_quant, 2)],
-        }
-
-        loads(8)
-        wh_regroup(0)
+        next_loads(IO_SLOTS)
+        regroup_weights(0)
         transposes(0, 0)
-        pv = small_vectors_pe()
+        early_t = bank(7, [P, P], BF16)
+        nc.tensor.transpose(early_t[:], early[:], ident_b[:])
         transposes(0, 1)
-        small_vectors(pv)
-        wh_quant(0)
-        exits(0)
-        loads(1)
+        nc.vector.tensor_copy(out=early_cols[:], in_=early_t[:, 0:16])
+        nc.vector.tensor_tensor(out=hi_lo[:], in0=early_cols[:, 12:14], in1=early_cols[:, 14:16], op=ALU.add)
+        nc.scalar.activation(out=exp_hi_lo[:], in_=hi_lo[:], func=ACT.Exp)
+        quantise_weights(0)
+        copy_out(0)
         transposes(1, 0)
         transposes(1, 1)
-        quant_h(0)
-        stage1(0)
-        loads(1)
-        exits(1)
-        for tick in range(NIT + 2):
-            ahead = tick + 2
-            if ahead < NIT:
-                transposes(ahead, 0)
-                transposes(ahead, 1)
-                loads(1)
-            if tick + 1 < NIT:
-                quant_h(tick + 1)
-            if tick < NIT:
-                silu(tick)
-            if tick + 1 < NIT:
-                stage1(tick + 1)
-            if 0 <= tick - 1 < NIT:
-                regroup_g(tick - 1)
-            if ahead < NIT:
-                exits(ahead)
-            for fn, arg in hooks.get(tick, []):
-                fn(arg)
-            if tick == 8:
-                load_late_vectors()
-            if tick == 12:
-                nc.vector.tensor_copy(out=bmu_f[:], in_=bmu_b[:])
-            if 0 <= tick - 1 < NIT:
-                quant_g(tick - 1)
-            if tick == 22:
-                pv2 = psum.tile([P, P], BF16, name="pv2", tag="b0")
-                nc.tensor.transpose(pv2[:], vecs2[:], ident_b[:])
-                nc.vector.tensor_copy(out=cols2[:], in_=pv2[:, 0:E])
+        quantise_h(0)
+        layer(0)
+        copy_out(1)
+        for r in range(NIT + 2):
+            if r + AHEAD < NIT:
+                transposes(r + AHEAD, 0)
+                transposes(r + AHEAD, 1)
+            if r + 1 < NIT:
+                quantise_h(r + 1)
+            if r < NIT:
+                swish(r)
+            if r + 1 < NIT:
+                layer(r + 1)
+            if 1 <= r <= NIT:
+                regroup_g(r - 1)
+            if r + AHEAD < NIT:
+                copy_out(r + AHEAD)
+            if r // 2 + 1 < 2 * E:
+                if r % 2 == 0:
+                    regroup_weights(r // 2 + 1)
+                else:
+                    quantise_weights(r // 2 + 1)
+            if 1 <= r <= NIT:
+                quantise_g(r - 1)
+            if r == 2 * 2 * E:
+                nc.sync.dma_start(out=bmu_bf[:], in_=bmu.rearrange("e o -> (e o)").partition_broadcast(P))
+                nc.sync.dma_start(out=late[0:E, :], in_=bsig)
+            if r == NIT - AHEAD:
+                nc.vector.tensor_copy(out=bmu_all[:], in_=bmu_bf[:])
+                late_t = bank(0, [P, P], BF16)
+                nc.tensor.transpose(late_t[:], late[:], ident_b[:])
+                nc.vector.tensor_copy(out=late_cols[:], in_=late_t[:, 0:E])
                 nc.vector.tensor_scalar(
-                    out=c2[:], in0=cols2[:], scalar1=2.0, scalar2=hl[:, 0:1],
+                    out=sig_bias[:], in0=late_cols[:], scalar1=2.0, scalar2=hi_lo[:, 0:1],
                     op0=ALU.mult, op1=ALU.subtract,
                 )
 
-        def sigma_head(i):
-            c, e = divmod(i, E)
-            pg = psum.tile([P, HID], F32, name="pg", tag="b%d" % (4 + i % 4))
+        def sigma_head(k):
+            c, e = divmod(k, E)
+            i = e * CH + c
+            raw = bank(4 + k % 4, [P, COLS])
             nc.tensor.matmul_mx(
-                out=pg[:],
-                lhsT=w2q[:, e, OD : 2 * OD].bitcast(FP8X4),
-                lhsT_scale=w2s[:, e, OD : 2 * OD],
-                rhs=gq[(c, e)][:].bitcast(FP8X4),
-                rhs_scale=gs[(c, e)][:],
+                out=raw[:],
+                lhsT=head_codes[:, e, OD : 2 * OD].bitcast(FP8X4),
+                lhsT_scale=head_scales[:, e, OD : 2 * OD],
+                rhs=g_codes[i][:].bitcast(FP8X4),
+                rhs_scale=g_scales[i][:],
                 start=True,
                 stop=True,
             )
-            sg[i] = keep.tile([P, HID], F32, name="sg%d" % i)
+            sg[k] = keep.tile([P, COLS], F32, name="sg%d" % k)
             nc.scalar.activation(
-                out=sg[i][:], in_=pg[:], func=ACT.Sigmoid, bias=c2[:, e : e + 1], scale=2.0
+                out=sg[k][:], in_=raw[:], func=ACT.Sigmoid, bias=sig_bias[:, e : e + 1], scale=2.0
             )
 
-        def mu_head(i):
-            c, e = divmod(i, E)
-            pm = psum.tile([P, SL, OD], F32, name="pm", tag="b%d" % (i % 4))
+        def mu_head(k):
+            c, e = divmod(k, E)
+            i = e * CH + c
+            mu = bank(k % 4, [P, SL, OD])
             for t in range(SL):
                 nc.tensor.matmul_mx(
-                    out=pm[:, t, :],
-                    lhsT=gq[(c, e)][:, t * P : (t + 1) * P].bitcast(FP8X4),
-                    lhsT_scale=gs[(c, e)][:, t * P : (t + 1) * P],
-                    rhs=w2q[:, e, 0:OD].bitcast(FP8X4),
-                    rhs_scale=w2s[:, e, 0:OD],
+                    out=mu[:, t, :],
+                    lhsT=g_codes[i][:, t * P : (t + 1) * P].bitcast(FP8X4),
+                    lhsT_scale=g_scales[i][:, t * P : (t + 1) * P],
+                    rhs=head_codes[:, e, 0:OD].bitcast(FP8X4),
+                    rhs_scale=head_scales[:, e, 0:OD],
                     start=True,
                     stop=True,
                 )
             if e == 0:
                 ds[c] = io.tile([P, SL, E * SD], F32, name="ds_mu", tag="io")
+                rw[c] = work.tile([P, SL, E, RD], F32, name="r_mu", tag="reward", bufs=CH)
+            bias = bmu_all[:, e * OD : (e + 1) * OD].unsqueeze(1)
             nc.vector.tensor_tensor(
-                out=ds[c][:, :, e * SD : (e + 1) * SD], in0=pm[:, :, 0:SD],
-                in1=bmu_f[:, e * OD : e * OD + SD].unsqueeze(1).to_broadcast([P, SL, SD]),
-                op=ALU.add,
+                out=ds[c][:, :, e * SD : (e + 1) * SD], in0=mu[:, :, 0:SD],
+                in1=bias[:, :, 0:SD].to_broadcast([P, SL, SD]), op=ALU.add,
             )
             nc.vector.tensor_tensor(
-                out=r_mu[:, c, :, e, :], in0=pm[:, :, SD:OD],
-                in1=bmu_f[:, e * OD + SD : (e + 1) * OD].unsqueeze(1).to_broadcast([P, SL, OD - SD]),
-                op=ALU.add,
+                out=rw[c][:, :, e, :], in0=mu[:, :, SD:OD],
+                in1=bias[:, :, SD:OD].to_broadcast([P, SL, RD]), op=ALU.add,
             )
             if e == E - 1:
-                nc.sync.dma_start(out=ds_mu_rows[c], in_=ds[c][:])
+                nc.sync.dma_start(out=ds_mu_view[c], in_=ds[c][:])
+                nc.sync.dma_start(out=r_mu_view[c], in_=rw[c][:].rearrange("p t e o -> p (t e o)"))
 
-        for i in range(NIT + 1):
-            if i < NIT:
-                sigma_head(i)
-            if i >= 1:
-                mu_head(i - 1)
-        nc.sync.dma_start(out=r_mu_rows, in_=r_mu[:].rearrange("p c t e o -> p c (t e o)"))
+        for k in range(NIT + 1):
+            if k < NIT:
+                sigma_head(k)
+            if k >= 1:
+                mu_head(k - 1)
 
-        r_sg_view = r_sg[:].rearrange("p c t e o -> p c (t e o)")
-        pt = {}
-
-        def sqrt_and_back(i):
+        def sqrt_and_back(k):
             nc.scalar.activation(
-                out=sg[i][:], in_=sg[i][:], func=ACT.Sqrt, bias=ab[:, 1:2], scale=ab[:, 0:1]
+                out=sg[k][:], in_=sg[k][:], func=ACT.Sqrt,
+                bias=exp_hi_lo[:, 1:2], scale=exp_hi_lo[:, 0:1],
             )
-            pt[i] = psum.tile([P, SL, OD], F32, name="pt", tag="b%d" % (i % 8))
+            back[k] = bank(k % 8, [P, SL, OD])
             for t in range(SL):
-                nc.tensor.transpose(pt[i][:, t, :], sg[i][:, t * P : (t + 1) * P], ident_f[:])
+                nc.tensor.transpose(back[k][:, t, :], sg[k][:, t * P : (t + 1) * P], ident_f[:])
 
-        def sigma_out(i):
-            c, e = divmod(i, E)
-            last = c == CH - 1
+        def sigma_out(k):
+            c, e = divmod(k, E)
+            first, members = 0, E
+            if c == CH - 1:
+                first, members = (0, E - 1) if e < E - 1 else (E - 1, 1)
+            if e == first:
+                ds[c] = io.tile([P, SL, members * SD], F32, name="ds_sg", tag="io")
             if e == 0:
-                ds[c] = io.tile([P, SL, (2 if last else E) * SD], F32, name="ds_sg", tag="io")
-            if last and e == E - 1:
-                ds[c] = io.tile([P, SL, SD], F32, name="ds_sg_end", tag="io")
-            col = 0 if (last and e == E - 1) else e * SD
-            copy = nc.scalar.copy if i in SCALAR_SIGMA_OUT else nc.vector.tensor_copy
-            copy(out=ds[c][:, :, col : col + SD], in_=pt[i][:, :, 0:SD])
-            copy(out=r_sg[:, c, :, e, :], in_=pt[i][:, :, SD:OD])
-            if not last and e == E - 1:
-                nc.sync.dma_start(out=ds_sg_rows[c], in_=ds[c][:])
-            if c == CH - 2 and e == E - 1:
-                nc.sync.dma_start(out=r_sg_rows[:, 0 : CH - 1], in_=r_sg_view[:, 0 : CH - 1])
-            if last and e == E - 2:
-                nc.sync.dma_start(out=ds_sg_rows[c][:, :, 0 : 2 * SD], in_=ds[c][:])
-            if last and e == E - 1:
-                nc.sync.dma_start(out=ds_sg_rows[c][:, :, 2 * SD : 3 * SD], in_=ds[c][:])
+                rw[c] = work.tile([P, SL, E, RD], F32, name="r_sg", tag="reward", bufs=CH)
+            nc.vector.tensor_copy(
+                out=ds[c][:, :, (e - first) * SD : (e - first + 1) * SD], in_=back[k][:, :, 0:SD]
+            )
+            nc.vector.tensor_copy(out=rw[c][:, :, e, :], in_=back[k][:, :, SD:OD])
+            if e == first + members - 1:
+                nc.sync.dma_start(
+                    out=ds_sg_view[c][:, :, first * SD : (first + members) * SD], in_=ds[c][:]
+                )
+            if e == E - 1:
+                nc.sync.dma_start(out=r_sg_view[c], in_=rw[c][:].rearrange("p t e o -> p (t e o)"))
 
-        for i in range(NIT + 2):
-            if i < NIT:
-                sqrt_and_back(i)
-            if i >= 2:
-                sigma_out(i - 2)
-        nc.sync.dma_start(out=r_sg_rows[:, CH - 1 : CH], in_=r_sg_view[:, CH - 1 : CH])
+        for k in range(NIT + 2):
+            if k < NIT:
+                sqrt_and_back(k)
+            if k >= 2:
+                sigma_out(k - 2)

@@ -19,10 +19,16 @@ CH = 8
 SL = N // (CH * P)
 COLS = SL * P
 NIT = CH * E
+WEIGHT_SETS = 2 * E
 AHEAD = 2
-IO_SLOTS = 9
+IO_SLOTS = 7
+WEIGHT_SLOTS = 3
+WORK_BUFS = 3
 VECTOR_ONLY = 3
 SCALAR_ONLY = 7
+MU_BEHIND = 1
+OUT_BEHIND = 2
+BOUND_ROW = E * PACK
 FLOPS = 2 * N * E * HID * (HID + 2 * OD)
 
 
@@ -35,7 +41,8 @@ def tile_ensembleenvprob_pa_t_kernel(
         const = ctx.enter_context(tc.tile_pool(name="const", bufs=1))
         keep = ctx.enter_context(tc.tile_pool(name="keep", bufs=1))
         io = ctx.enter_context(tc.tile_pool(name="io", bufs=IO_SLOTS))
-        work = ctx.enter_context(tc.tile_pool(name="work", bufs=3))
+        weights = ctx.enter_context(tc.tile_pool(name="weights", bufs=WEIGHT_SLOTS))
+        work = ctx.enter_context(tc.tile_pool(name="work", bufs=WORK_BUFS))
         psum = ctx.enter_context(tc.psum_pool(name="psum", bufs=1))
         ctx.enter_context(tc.manual_schedule())
 
@@ -56,11 +63,10 @@ def tile_ensembleenvprob_pa_t_kernel(
         nc.vector.memset(early[:], 0.0)
         late = const.tile([P, P], BF16, name="late")
         nc.vector.memset(late[:], 0.0)
-        nc.scalar.dma_start(out=early[0 : E * PACK, :], in_=bh.rearrange("e (j p) -> (e j) p", p=P))
-        nc.scalar.dma_start(out=early[12:13, 0:SD], in_=max_lv_s)
-        nc.scalar.dma_start(out=early[13:14, 0:SD], in_=min_lv_s)
-        nc.scalar.dma_start(out=early[14:15, SD:OD], in_=max_lv_r)
-        nc.scalar.dma_start(out=early[15:16, SD:OD], in_=min_lv_r)
+        nc.scalar.dma_start(out=early[0:BOUND_ROW, :], in_=bh.rearrange("e (j p) -> (e j) p", p=P))
+        bounds = ((max_lv_s, 0, SD), (min_lv_s, 0, SD), (max_lv_r, SD, OD), (min_lv_r, SD, OD))
+        for k, (bound, start, stop) in enumerate(bounds):
+            nc.scalar.dma_start(out=early[BOUND_ROW + k : BOUND_ROW + k + 1, start:stop], in_=bound)
 
         wh_codes = const.tile([P, E, HID], U32, name="wh_codes", align_bytes=64)
         wh_scales = const.tile([P, E, HID], U8, name="wh_scales", align_bytes=64)
@@ -68,7 +74,7 @@ def tile_ensembleenvprob_pa_t_kernel(
         head_scales = const.tile([P, E, 2 * OD], U8, name="head_scales", align_bytes=64)
         bmu_bf = const.tile([P, E * OD], BF16, name="bmu_bf")
         bmu_all = const.tile([P, E * OD], F32, name="bmu_all")
-        early_cols = const.tile([P, 16], F32, name="early_cols")
+        early_cols = const.tile([P, BOUND_ROW + 4], F32, name="early_cols")
         late_cols = const.tile([P, E], F32, name="late_cols")
         hi_lo = const.tile([P, 2], F32, name="hi_lo")
         exp_hi_lo = const.tile([P, 2], F32, name="exp_hi_lo")
@@ -76,7 +82,7 @@ def tile_ensembleenvprob_pa_t_kernel(
 
         h_sb, w_raw, w_grouped = {}, {}, {}
         xt, h_grouped, h_codes, h_scales, acc, g_planes, g_grouped = {}, {}, {}, {}, {}, {}, {}
-        g_codes, g_scales, sg, back, ds, rw = {}, {}, {}, {}, {}, {}
+        g_codes, g_scales, sigma_t, back, state, reward = {}, {}, {}, {}, {}, {}
 
         def member_chunk(i):
             return i // CH, i % CH
@@ -92,33 +98,18 @@ def tile_ensembleenvprob_pa_t_kernel(
 
         def load_weights(w):
             if w < E:
-                w_raw[w] = io.tile([P, PACK, HID], BF16, name="w_raw", tag="io")
+                w_raw[w] = weights.tile([P, PACK, HID], BF16, name="w_raw", tag="w_raw")
                 nc.sync.dma_start(
                     out=w_raw[w][:].rearrange("p (u a) f -> p u (a f)", u=2),
                     in_=Wh[w].rearrange("(u p a) f -> p u (a f)", u=2, a=2),
                 )
             else:
-                w_raw[w] = io.tile([P, PACK, 2 * OD], BF16, name="w_raw", tag="io")
+                w_raw[w] = weights.tile([P, PACK, 2 * OD], BF16, name="w_raw", tag="w_raw")
                 for m, head in enumerate((Wmu, Wsig)):
                     nc.sync.dma_start(
                         out=w_raw[w][:, :, m * OD : (m + 1) * OD],
                         in_=head[w - E].rearrange("(j p) o -> p j o", p=P),
                     )
-
-        load_order = [("w", 0), ("h", 0)]
-        for i in range(1, NIT):
-            load_order.append(("h", i))
-            if i < 2 * E:
-                load_order.append(("w", i))
-        issued = [0]
-
-        def next_loads(count):
-            for kind, k in load_order[issued[0] : issued[0] + count]:
-                if kind == "w":
-                    load_weights(k)
-                else:
-                    load_h(k)
-            issued[0] += count
 
         def regroup(dst, src):
             nc.vector.tensor_copy(
@@ -130,7 +121,8 @@ def tile_ensembleenvprob_pa_t_kernel(
             width = HID if w < E else 2 * OD
             w_grouped[w] = work.tile([P, PACK * width], BF16, name="w_grouped", tag="grouped", align_bytes=64)
             regroup(w_grouped[w][:], w_raw[w][:])
-            next_loads(1)
+            if w + WEIGHT_SLOTS < WEIGHT_SETS:
+                load_weights(w + WEIGHT_SLOTS)
 
         def quantise_weights(w):
             codes, scales = (wh_codes, wh_scales) if w < E else (head_codes, head_scales)
@@ -149,8 +141,8 @@ def tile_ensembleenvprob_pa_t_kernel(
                         words[:, base + u * P : base + (u + 1) * P],
                         ident_f[:],
                     )
-            if half == 1:
-                next_loads(1)
+            if half == 1 and i + IO_SLOTS < NIT:
+                load_h(i + IO_SLOTS)
 
         def copy_out(i):
             for half in range(2):
@@ -210,14 +202,24 @@ def tile_ensembleenvprob_pa_t_kernel(
                 out=g_codes[i][:].bitcast(FP8X4), scales=g_scales[i][:], in_=g_grouped[i][:]
             )
 
-        next_loads(IO_SLOTS)
+        load_weights(0)
+        load_h(0)
+        load_h(1)
+        load_weights(1)
+        load_h(2)
+        load_weights(2)
+        for i in range(3, IO_SLOTS):
+            load_h(i)
         regroup_weights(0)
         transposes(0, 0)
         early_t = bank(7, [P, P], BF16)
         nc.tensor.transpose(early_t[:], early[:], ident_b[:])
         transposes(0, 1)
-        nc.vector.tensor_copy(out=early_cols[:], in_=early_t[:, 0:16])
-        nc.vector.tensor_tensor(out=hi_lo[:], in0=early_cols[:, 12:14], in1=early_cols[:, 14:16], op=ALU.add)
+        nc.vector.tensor_copy(out=early_cols[:], in_=early_t[:, 0 : BOUND_ROW + 4])
+        nc.vector.tensor_tensor(
+            out=hi_lo[:], in0=early_cols[:, BOUND_ROW : BOUND_ROW + 2],
+            in1=early_cols[:, BOUND_ROW + 2 : BOUND_ROW + 4], op=ALU.add,
+        )
         nc.scalar.activation(out=exp_hi_lo[:], in_=hi_lo[:], func=ACT.Exp)
         quantise_weights(0)
         copy_out(0)
@@ -240,14 +242,14 @@ def tile_ensembleenvprob_pa_t_kernel(
                 regroup_g(r - 1)
             if r + AHEAD < NIT:
                 copy_out(r + AHEAD)
-            if r // 2 + 1 < 2 * E:
+            if r // 2 + 1 < WEIGHT_SETS:
                 if r % 2 == 0:
                     regroup_weights(r // 2 + 1)
                 else:
                     quantise_weights(r // 2 + 1)
             if 1 <= r <= NIT:
                 quantise_g(r - 1)
-            if r == 2 * 2 * E:
+            if r == 2 * WEIGHT_SETS:
                 nc.sync.dma_start(out=bmu_bf[:], in_=bmu.rearrange("e o -> (e o)").partition_broadcast(P))
                 nc.sync.dma_start(out=late[0:E, :], in_=bsig)
             if r == NIT - AHEAD:
@@ -273,9 +275,9 @@ def tile_ensembleenvprob_pa_t_kernel(
                 start=True,
                 stop=True,
             )
-            sg[k] = keep.tile([P, COLS], F32, name="sg%d" % k)
+            sigma_t[k] = keep.tile([P, COLS], F32, name="sg%d" % k)
             nc.scalar.activation(
-                out=sg[k][:], in_=raw[:], func=ACT.Sigmoid, bias=sig_bias[:, e : e + 1], scale=2.0
+                out=sigma_t[k][:], in_=raw[:], func=ACT.Sigmoid, bias=sig_bias[:, e : e + 1], scale=2.0
             )
 
         def mu_head(k):
@@ -293,35 +295,35 @@ def tile_ensembleenvprob_pa_t_kernel(
                     stop=True,
                 )
             if e == 0:
-                ds[c] = io.tile([P, SL, E * SD], F32, name="ds_mu", tag="io")
-                rw[c] = work.tile([P, SL, E, RD], F32, name="r_mu", tag="reward", bufs=CH)
+                state[c] = io.tile([P, SL, E * SD], F32, name="ds_mu", tag="io")
+                reward[c] = work.tile([P, SL, E, RD], F32, name="r_mu", tag="reward", bufs=CH)
             bias = bmu_all[:, e * OD : (e + 1) * OD].unsqueeze(1)
             nc.vector.tensor_tensor(
-                out=ds[c][:, :, e * SD : (e + 1) * SD], in0=mu[:, :, 0:SD],
+                out=state[c][:, :, e * SD : (e + 1) * SD], in0=mu[:, :, 0:SD],
                 in1=bias[:, :, 0:SD].to_broadcast([P, SL, SD]), op=ALU.add,
             )
             nc.vector.tensor_tensor(
-                out=rw[c][:, :, e, :], in0=mu[:, :, SD:OD],
+                out=reward[c][:, :, e, :], in0=mu[:, :, SD:OD],
                 in1=bias[:, :, SD:OD].to_broadcast([P, SL, RD]), op=ALU.add,
             )
             if e == E - 1:
-                nc.sync.dma_start(out=ds_mu_view[c], in_=ds[c][:])
-                nc.sync.dma_start(out=r_mu_view[c], in_=rw[c][:].rearrange("p t e o -> p (t e o)"))
+                nc.sync.dma_start(out=ds_mu_view[c], in_=state[c][:])
+                nc.sync.dma_start(out=r_mu_view[c], in_=reward[c][:].rearrange("p t e o -> p (t e o)"))
 
-        for k in range(NIT + 1):
+        for k in range(NIT + MU_BEHIND):
             if k < NIT:
                 sigma_head(k)
-            if k >= 1:
-                mu_head(k - 1)
+            if k >= MU_BEHIND:
+                mu_head(k - MU_BEHIND)
 
         def sqrt_and_back(k):
             nc.scalar.activation(
-                out=sg[k][:], in_=sg[k][:], func=ACT.Sqrt,
+                out=sigma_t[k][:], in_=sigma_t[k][:], func=ACT.Sqrt,
                 bias=exp_hi_lo[:, 1:2], scale=exp_hi_lo[:, 0:1],
             )
             back[k] = bank(k % 8, [P, SL, OD])
             for t in range(SL):
-                nc.tensor.transpose(back[k][:, t, :], sg[k][:, t * P : (t + 1) * P], ident_f[:])
+                nc.tensor.transpose(back[k][:, t, :], sigma_t[k][:, t * P : (t + 1) * P], ident_f[:])
 
         def sigma_out(k):
             c, e = divmod(k, E)
@@ -329,22 +331,22 @@ def tile_ensembleenvprob_pa_t_kernel(
             if c == CH - 1:
                 first, members = (0, E - 1) if e < E - 1 else (E - 1, 1)
             if e == first:
-                ds[c] = io.tile([P, SL, members * SD], F32, name="ds_sg", tag="io")
+                state[c] = io.tile([P, SL, members * SD], F32, name="ds_sg", tag="io")
             if e == 0:
-                rw[c] = work.tile([P, SL, E, RD], F32, name="r_sg", tag="reward", bufs=CH)
+                reward[c] = work.tile([P, SL, E, RD], F32, name="r_sg", tag="reward", bufs=CH)
             nc.vector.tensor_copy(
-                out=ds[c][:, :, (e - first) * SD : (e - first + 1) * SD], in_=back[k][:, :, 0:SD]
+                out=state[c][:, :, (e - first) * SD : (e - first + 1) * SD], in_=back[k][:, :, 0:SD]
             )
-            nc.vector.tensor_copy(out=rw[c][:, :, e, :], in_=back[k][:, :, SD:OD])
+            nc.vector.tensor_copy(out=reward[c][:, :, e, :], in_=back[k][:, :, SD:OD])
             if e == first + members - 1:
                 nc.sync.dma_start(
-                    out=ds_sg_view[c][:, :, first * SD : (first + members) * SD], in_=ds[c][:]
+                    out=ds_sg_view[c][:, :, first * SD : (first + members) * SD], in_=state[c][:]
                 )
             if e == E - 1:
-                nc.sync.dma_start(out=r_sg_view[c], in_=rw[c][:].rearrange("p t e o -> p (t e o)"))
+                nc.sync.dma_start(out=r_sg_view[c], in_=reward[c][:].rearrange("p t e o -> p (t e o)"))
 
-        for k in range(NIT + 2):
+        for k in range(NIT + OUT_BEHIND):
             if k < NIT:
                 sqrt_and_back(k)
-            if k >= 2:
-                sigma_out(k - 2)
+            if k >= OUT_BEHIND:
+                sigma_out(k - OUT_BEHIND)

@@ -1,3 +1,4 @@
+import math
 from contextlib import ExitStack
 
 import concourse.mybir as mybir
@@ -21,14 +22,15 @@ COLS = SL * P
 NIT = CH * E
 WEIGHT_SETS = 2 * E
 AHEAD = 2
-IO_SLOTS = 7
+IO_SLOTS = 6
 WEIGHT_SLOTS = 3
 WORK_BUFS = 3
-VECTOR_ONLY = 3
-SCALAR_ONLY = 7
-MU_BEHIND = 1
-OUT_BEHIND = 2
-BOUND_ROW = E * PACK
+GROUP = CH // 2
+HEADS_FROM = GROUP * E
+EARLY = NIT - HEADS_FROM
+SCALAR_ONLY = 2 * WEIGHT_SETS
+BOUND_ROW = E
+LOG2_E = 1.0 / math.log(2.0)
 FLOPS = 2 * N * E * HID * (HID + 2 * OD)
 
 
@@ -41,6 +43,7 @@ def tile_ensembleenvprob_pa_t_kernel(
         const = ctx.enter_context(tc.tile_pool(name="const", bufs=1))
         keep = ctx.enter_context(tc.tile_pool(name="keep", bufs=1))
         io = ctx.enter_context(tc.tile_pool(name="io", bufs=IO_SLOTS))
+        early_out = ctx.enter_context(tc.tile_pool(name="early_out", bufs=2))
         weights = ctx.enter_context(tc.tile_pool(name="weights", bufs=WEIGHT_SLOTS))
         work = ctx.enter_context(tc.tile_pool(name="work", bufs=WORK_BUFS))
         psum = ctx.enter_context(tc.psum_pool(name="psum", bufs=1))
@@ -61,12 +64,13 @@ def tile_ensembleenvprob_pa_t_kernel(
         make_identity(nc, ident_b[:])
         early = const.tile([P, P], BF16, name="early")
         nc.vector.memset(early[:], 0.0)
+        warm = const.tile([P, 1], F32, name="warm")
+        nc.vector.memset(warm[:], 0.0)
+        nc.scalar.activation(out=warm[:], in_=warm[:], func=ACT.Silu)
         late = const.tile([P, P], BF16, name="late")
-        nc.vector.memset(late[:], 0.0)
-        nc.scalar.dma_start(out=early[0:BOUND_ROW, :], in_=bh.rearrange("e (j p) -> (e j) p", p=P))
-        bounds = ((max_lv_s, 0, SD), (min_lv_s, 0, SD), (max_lv_r, SD, OD), (min_lv_r, SD, OD))
-        for k, (bound, start, stop) in enumerate(bounds):
-            nc.scalar.dma_start(out=early[BOUND_ROW + k : BOUND_ROW + k + 1, start:stop], in_=bound)
+        nc.gpsimd.memset(late[:], 0.0)
+        twos = const.tile([P, 2], F32, name="twos")
+        nc.gpsimd.memset(twos[:], 2.0)
 
         wh_codes = const.tile([P, E, HID], U32, name="wh_codes", align_bytes=64)
         wh_scales = const.tile([P, E, HID], U8, name="wh_scales", align_bytes=64)
@@ -74,18 +78,27 @@ def tile_ensembleenvprob_pa_t_kernel(
         head_scales = const.tile([P, E, 2 * OD], U8, name="head_scales", align_bytes=64)
         bmu_bf = const.tile([P, E * OD], BF16, name="bmu_bf")
         bmu_all = const.tile([P, E * OD], F32, name="bmu_all")
-        early_cols = const.tile([P, BOUND_ROW + 4], F32, name="early_cols")
-        late_cols = const.tile([P, E], F32, name="late_cols")
+        early_cols = const.tile([P, E * PACK], F32, name="early_cols")
+        late_cols = const.tile([P, BOUND_ROW + 4], F32, name="late_cols")
         hi_lo = const.tile([P, 2], F32, name="hi_lo")
+        log2_hi_lo = const.tile([P, 2], F32, name="log2_hi_lo")
         exp_hi_lo = const.tile([P, 2], F32, name="exp_hi_lo")
+        half_hi = const.tile([P, 1], F32, name="half_hi")
         sig_bias = const.tile([P, E], F32, name="sig_bias")
+        slope = const.tile([P, 1], F32, name="slope")
+        offset = const.tile([P, 1], F32, name="offset")
 
         h_sb, w_raw, w_grouped = {}, {}, {}
         xt, h_grouped, h_codes, h_scales, acc, g_planes, g_grouped = {}, {}, {}, {}, {}, {}, {}
-        g_codes, g_scales, sigma_t, back, state, reward = {}, {}, {}, {}, {}, {}
+        g_codes, g_scales, sigma_t, state, reward = {}, {}, {}, {}, {}
 
         def member_chunk(i):
-            return i // CH, i % CH
+            half, rest = divmod(i, GROUP * E)
+            return rest // GROUP, half * GROUP + rest % GROUP
+
+        def iteration(k):
+            c, e = divmod(k, E)
+            return (c // GROUP) * GROUP * E + e * GROUP + c % GROUP
 
         def load_h(i):
             e, c = member_chunk(i)
@@ -151,7 +164,7 @@ def tile_ensembleenvprob_pa_t_kernel(
                 )
                 dst = h_grouped[(i, half)][:].rearrange("p (n u) -> p n u", u=2)
                 src = xt[(i, half)][:].rearrange("p u n -> p n u")
-                on_scalar = (half == 0 and i >= VECTOR_ONLY) or VECTOR_ONLY <= i < SCALAR_ONLY
+                on_scalar = i != 1 and (half == 0 or i < SCALAR_ONLY)
                 if on_scalar:
                     nc.scalar.copy(out=dst, in_=src)
                 else:
@@ -202,8 +215,65 @@ def tile_ensembleenvprob_pa_t_kernel(
                 out=g_codes[i][:].bitcast(FP8X4), scales=g_scales[i][:], in_=g_grouped[i][:]
             )
 
+        def mu_head(k, bank_no):
+            c, e = divmod(k, E)
+            i = iteration(k)
+            mu = bank(bank_no, [P, SL, OD])
+            for t in range(SL):
+                nc.tensor.matmul_mx(
+                    out=mu[:, t, :],
+                    lhsT=g_codes[i][:, t * P : (t + 1) * P].bitcast(FP8X4),
+                    lhsT_scale=g_scales[i][:, t * P : (t + 1) * P],
+                    rhs=head_codes[:, e, 0:OD].bitcast(FP8X4),
+                    rhs_scale=head_scales[:, e, 0:OD],
+                    start=True,
+                    stop=True,
+                )
+            if e == 0:
+                pool, tag = (early_out, "early_out") if k < EARLY else (io, "io")
+                state[("mu", c)] = pool.tile([P, SL, E * SD], F32, name="ds_mu", tag=tag)
+                reward[("mu", c)] = work.tile([P, SL, E, RD], F32, name="r_mu", tag="reward", bufs=CH)
+            bias = bmu_all[:, e * OD : (e + 1) * OD].unsqueeze(1)
+            nc.vector.tensor_tensor(
+                out=state[("mu", c)][:, :, e * SD : (e + 1) * SD], in0=mu[:, :, 0:SD],
+                in1=bias[:, :, 0:SD].to_broadcast([P, SL, SD]), op=ALU.add,
+            )
+            nc.vector.tensor_tensor(
+                out=reward[("mu", c)][:, :, e, :], in0=mu[:, :, SD:OD],
+                in1=bias[:, :, SD:OD].to_broadcast([P, SL, RD]), op=ALU.add,
+            )
+            if e == E - 1:
+                nc.sync.dma_start(out=ds_mu_view[c], in_=state[("mu", c)][:])
+                nc.sync.dma_start(
+                    out=r_mu_view[c], in_=reward[("mu", c)][:].rearrange("p t e o -> p (t e o)")
+                )
+
+        def sigma_head(k, bank_no):
+            e, i = k % E, iteration(k)
+            raw = bank(bank_no, [P, COLS])
+            nc.tensor.matmul_mx(
+                out=raw[:],
+                lhsT=head_codes[:, e, OD : 2 * OD].bitcast(FP8X4),
+                lhsT_scale=head_scales[:, e, OD : 2 * OD],
+                rhs=g_codes[i][:].bitcast(FP8X4),
+                rhs_scale=g_scales[i][:],
+                start=True,
+                stop=True,
+            )
+            sigma_t[k] = keep.tile([P, COLS], F32, name="sg%d" % k)
+            nc.scalar.activation(
+                out=sigma_t[k][:], in_=raw[:], func=ACT.Tanh, bias=sig_bias[:, e : e + 1], scale=1.0
+            )
+
+        def sigma_square(k):
+            nc.gpsimd.tensor_scalar(
+                out=sigma_t[k][:], in0=sigma_t[k][:], scalar1=slope[:], scalar2=offset[:],
+                op0=ALU.mult, op1=ALU.add,
+            )
+
         load_weights(0)
         load_h(0)
+        nc.sync.dma_start(out=early[0 : E * PACK, :], in_=bh.rearrange("e (j p) -> (e j) p", p=P))
         load_h(1)
         load_weights(1)
         load_h(2)
@@ -212,22 +282,18 @@ def tile_ensembleenvprob_pa_t_kernel(
             load_h(i)
         regroup_weights(0)
         transposes(0, 0)
-        early_t = bank(7, [P, P], BF16)
-        nc.tensor.transpose(early_t[:], early[:], ident_b[:])
         transposes(0, 1)
-        nc.vector.tensor_copy(out=early_cols[:], in_=early_t[:, 0 : BOUND_ROW + 4])
-        nc.vector.tensor_tensor(
-            out=hi_lo[:], in0=early_cols[:, BOUND_ROW : BOUND_ROW + 2],
-            in1=early_cols[:, BOUND_ROW + 2 : BOUND_ROW + 4], op=ALU.add,
-        )
-        nc.scalar.activation(out=exp_hi_lo[:], in_=hi_lo[:], func=ACT.Exp)
         quantise_weights(0)
         copy_out(0)
         transposes(1, 0)
         transposes(1, 1)
+        early_t = bank(7, [P, P], BF16)
+        nc.tensor.transpose(early_t[:], early[:], ident_b[:])
         quantise_h(0)
+        nc.vector.tensor_copy(out=early_cols[:], in_=early_t[:, 0 : E * PACK])
         layer(0)
         copy_out(1)
+        sigma_done, mu_done = 0, 0
         for r in range(NIT + 2):
             if r + AHEAD < NIT:
                 transposes(r + AHEAD, 0)
@@ -236,6 +302,18 @@ def tile_ensembleenvprob_pa_t_kernel(
                 quantise_h(r + 1)
             if r < NIT:
                 swish(r)
+            if r == NIT:
+                for k in range(EARLY):
+                    sigma_square(k)
+            if r >= HEADS_FROM:
+                for step in range(1 if r < NIT else 4):
+                    sigma_head(sigma_done, 2 * ((r + 1) % 2) + 1 if r < NIT else 4 + sigma_done % 4)
+                    if r >= NIT:
+                        sigma_square(sigma_done)
+                    sigma_done += 1
+                for step in range(1 if r + 1 < NIT else 2 if r <= NIT else 0):
+                    mu_head(mu_done, bank_no=2 * ((mu_done + 1) % 2) if r < NIT else mu_done % 4)
+                    mu_done += 1
             if r + 1 < NIT:
                 layer(r + 1)
             if 1 <= r <= NIT:
@@ -249,104 +327,68 @@ def tile_ensembleenvprob_pa_t_kernel(
                     quantise_weights(r // 2 + 1)
             if 1 <= r <= NIT:
                 quantise_g(r - 1)
-            if r == 2 * WEIGHT_SETS:
+            if r == WEIGHT_SETS:
                 nc.sync.dma_start(out=bmu_bf[:], in_=bmu.rearrange("e o -> (e o)").partition_broadcast(P))
                 nc.sync.dma_start(out=late[0:E, :], in_=bsig)
-            if r == NIT - AHEAD:
+                bounds = ((max_lv_s, 0, SD), (min_lv_s, 0, SD), (max_lv_r, SD, OD), (min_lv_r, SD, OD))
+                for k, (bound, start, stop) in enumerate(bounds):
+                    nc.sync.dma_start(out=late[BOUND_ROW + k : BOUND_ROW + k + 1, start:stop], in_=bound)
+            if r == HEADS_FROM - 1:
                 nc.vector.tensor_copy(out=bmu_all[:], in_=bmu_bf[:])
-                late_t = bank(0, [P, P], BF16)
+                late_t = bank(2 * ((r + 1) % 2), [P, P], BF16)
                 nc.tensor.transpose(late_t[:], late[:], ident_b[:])
-                nc.vector.tensor_copy(out=late_cols[:], in_=late_t[:, 0:E])
+                nc.vector.tensor_copy(out=late_cols[:], in_=late_t[:, 0 : BOUND_ROW + 4])
+                nc.vector.tensor_tensor(
+                    out=hi_lo[:], in0=late_cols[:, BOUND_ROW : BOUND_ROW + 2],
+                    in1=late_cols[:, BOUND_ROW + 2 : BOUND_ROW + 4], op=ALU.add,
+                )
+                nc.gpsimd.tensor_scalar(
+                    out=half_hi[:], in0=hi_lo[:, 0:1], scalar1=0.5, scalar2=0.0, op0=ALU.mult, op1=ALU.add
+                )
                 nc.vector.tensor_scalar(
-                    out=sig_bias[:], in0=late_cols[:], scalar1=2.0, scalar2=hi_lo[:, 0:1],
-                    op0=ALU.mult, op1=ALU.subtract,
+                    out=sig_bias[:], in0=late_cols[:, 0:E], scalar1=half_hi[:], scalar2=None, op0=ALU.subtract
                 )
-
-        def sigma_head(k):
-            c, e = divmod(k, E)
-            i = e * CH + c
-            raw = bank(4 + k % 4, [P, COLS])
-            nc.tensor.matmul_mx(
-                out=raw[:],
-                lhsT=head_codes[:, e, OD : 2 * OD].bitcast(FP8X4),
-                lhsT_scale=head_scales[:, e, OD : 2 * OD],
-                rhs=g_codes[i][:].bitcast(FP8X4),
-                rhs_scale=g_scales[i][:],
-                start=True,
-                stop=True,
-            )
-            sigma_t[k] = keep.tile([P, COLS], F32, name="sg%d" % k)
-            nc.scalar.activation(
-                out=sigma_t[k][:], in_=raw[:], func=ACT.Sigmoid, bias=sig_bias[:, e : e + 1], scale=2.0
-            )
-
-        def mu_head(k):
-            c, e = divmod(k, E)
-            i = e * CH + c
-            mu = bank(k % 4, [P, SL, OD])
-            for t in range(SL):
-                nc.tensor.matmul_mx(
-                    out=mu[:, t, :],
-                    lhsT=g_codes[i][:, t * P : (t + 1) * P].bitcast(FP8X4),
-                    lhsT_scale=g_scales[i][:, t * P : (t + 1) * P],
-                    rhs=head_codes[:, e, 0:OD].bitcast(FP8X4),
-                    rhs_scale=head_scales[:, e, 0:OD],
-                    start=True,
-                    stop=True,
+                nc.gpsimd.tensor_scalar(
+                    out=log2_hi_lo[:], in0=hi_lo[:], scalar1=LOG2_E, scalar2=0.0, op0=ALU.mult, op1=ALU.add
                 )
-            if e == 0:
-                state[c] = io.tile([P, SL, E * SD], F32, name="ds_mu", tag="io")
-                reward[c] = work.tile([P, SL, E, RD], F32, name="r_mu", tag="reward", bufs=CH)
-            bias = bmu_all[:, e * OD : (e + 1) * OD].unsqueeze(1)
-            nc.vector.tensor_tensor(
-                out=state[c][:, :, e * SD : (e + 1) * SD], in0=mu[:, :, 0:SD],
-                in1=bias[:, :, 0:SD].to_broadcast([P, SL, SD]), op=ALU.add,
-            )
-            nc.vector.tensor_tensor(
-                out=reward[c][:, :, e, :], in0=mu[:, :, SD:OD],
-                in1=bias[:, :, SD:OD].to_broadcast([P, SL, RD]), op=ALU.add,
-            )
-            if e == E - 1:
-                nc.sync.dma_start(out=ds_mu_view[c], in_=state[c][:])
-                nc.sync.dma_start(out=r_mu_view[c], in_=reward[c][:].rearrange("p t e o -> p (t e o)"))
-
-        for k in range(NIT + MU_BEHIND):
-            if k < NIT:
-                sigma_head(k)
-            if k >= MU_BEHIND:
-                mu_head(k - MU_BEHIND)
-
-        def sqrt_and_back(k):
-            nc.scalar.activation(
-                out=sigma_t[k][:], in_=sigma_t[k][:], func=ACT.Sqrt,
-                bias=exp_hi_lo[:, 1:2], scale=exp_hi_lo[:, 0:1],
-            )
-            back[k] = bank(k % 8, [P, SL, OD])
-            for t in range(SL):
-                nc.tensor.transpose(back[k][:, t, :], sigma_t[k][:, t * P : (t + 1) * P], ident_f[:])
+                nc.gpsimd.tensor_tensor(out=exp_hi_lo[:], in0=twos[:], in1=log2_hi_lo[:], op=ALU.pow)
+                nc.gpsimd.tensor_scalar(
+                    out=slope[:], in0=exp_hi_lo[:, 0:1], scalar1=0.5, scalar2=0.0, op0=ALU.mult, op1=ALU.add
+                )
+                nc.gpsimd.tensor_tensor(out=offset[:], in0=slope[:], in1=exp_hi_lo[:, 1:2], op=ALU.add)
 
         def sigma_out(k):
             c, e = divmod(k, E)
+            back = bank(4 + k % 4, [P, SL, OD])
+            for t in range(SL):
+                nc.tensor.transpose(back[:, t, :], sigma_t[k][:, t * P : (t + 1) * P], ident_f[:])
             first, members = 0, E
             if c == CH - 1:
                 first, members = (0, E - 1) if e < E - 1 else (E - 1, 1)
             if e == first:
-                state[c] = io.tile([P, SL, members * SD], F32, name="ds_sg", tag="io")
+                state[("sg", c)] = io.tile([P, SL, members * SD], F32, name="ds_sg", tag="io")
             if e == 0:
-                reward[c] = work.tile([P, SL, E, RD], F32, name="r_sg", tag="reward", bufs=CH)
-            nc.vector.tensor_copy(
-                out=state[c][:, :, (e - first) * SD : (e - first + 1) * SD], in_=back[k][:, :, 0:SD]
+                reward[("sg", c)] = work.tile([P, SL, E, RD], F32, name="r_sg", tag="reward", bufs=CH)
+            nc.scalar.activation(
+                out=state[("sg", c)][:, :, (e - first) * SD : (e - first + 1) * SD],
+                in_=back[:, :, 0:SD], func=ACT.Sqrt,
             )
-            nc.vector.tensor_copy(out=reward[c][:, :, e, :], in_=back[k][:, :, SD:OD])
+            nc.scalar.activation(out=reward[("sg", c)][:, :, e, :], in_=back[:, :, SD:OD], func=ACT.Sqrt)
             if e == first + members - 1:
                 nc.sync.dma_start(
-                    out=ds_sg_view[c][:, :, first * SD : (first + members) * SD], in_=state[c][:]
+                    out=ds_sg_view[c][:, :, first * SD : (first + members) * SD], in_=state[("sg", c)][:]
                 )
             if e == E - 1:
-                nc.sync.dma_start(out=r_sg_view[c], in_=reward[c][:].rearrange("p t e o -> p (t e o)"))
+                nc.sync.dma_start(
+                    out=r_sg_view[c], in_=reward[("sg", c)][:].rearrange("p t e o -> p (t e o)")
+                )
 
-        for k in range(NIT + OUT_BEHIND):
-            if k < NIT:
-                sqrt_and_back(k)
-            if k >= OUT_BEHIND:
-                sigma_out(k - OUT_BEHIND)
+        for k in range(sigma_done, NIT):
+            sigma_head(k, 4 + k % 4)
+            sigma_square(k)
+        for k in range(NIT):
+            for step in range(4 if k == 0 else k % 2):
+                if mu_done < NIT:
+                    mu_head(mu_done, bank_no=mu_done % 4)
+                    mu_done += 1
+            sigma_out(k)

@@ -158,11 +158,9 @@ def tile_ensembleenvprob_pa_t_kernel(
                 load_h(i + IO_SLOTS)
 
         def copy_out(i):
+            h_grouped[i] = work.tile([P, 2 * HID], F32, name="h_grouped", tag="h_grouped", align_bytes=64)
             for half in range(2):
-                h_grouped[(i, half)] = work.tile(
-                    [P, HID], F32, name="h_grouped", tag="h_grouped%d" % half, align_bytes=64
-                )
-                dst = h_grouped[(i, half)][:].rearrange("p (n u) -> p n u", u=2)
+                dst = h_grouped[i][:, half * HID : (half + 1) * HID].rearrange("p (n u) -> p n u", u=2)
                 src = xt[(i, half)][:].rearrange("p u n -> p n u")
                 on_scalar = i != 1 and (half == 0 or i < SCALAR_ONLY)
                 if on_scalar:
@@ -173,13 +171,9 @@ def tile_ensembleenvprob_pa_t_kernel(
         def quantise_h(i):
             h_codes[i] = work.tile([P, COLS], U32, name="h_codes", tag="h_codes", align_bytes=64)
             h_scales[i] = work.tile([P, COLS], U8, name="h_scales", tag="h_scales", align_bytes=64)
-            for half in range(2):
-                cols = slice(half * COLS // 2, (half + 1) * COLS // 2)
-                nc.vector.quantize_mx(
-                    out=h_codes[i][:, cols].bitcast(FP8X4),
-                    scales=h_scales[i][:, cols],
-                    in_=h_grouped[(i, half)][:].bitcast(BF16),
-                )
+            nc.vector.quantize_mx(
+                out=h_codes[i][:].bitcast(FP8X4), scales=h_scales[i][:], in_=h_grouped[i][:].bitcast(BF16)
+            )
 
         def layer(i):
             e = member_chunk(i)[0]
@@ -283,14 +277,14 @@ def tile_ensembleenvprob_pa_t_kernel(
         regroup_weights(0)
         transposes(0, 0)
         transposes(0, 1)
+        early_t = bank(7, [P, P], BF16)
+        nc.tensor.transpose(early_t[:], early[:], ident_b[:])
         quantise_weights(0)
+        nc.vector.tensor_copy(out=early_cols[:], in_=early_t[:, 0 : E * PACK])
         copy_out(0)
         transposes(1, 0)
         transposes(1, 1)
-        early_t = bank(7, [P, P], BF16)
-        nc.tensor.transpose(early_t[:], early[:], ident_b[:])
         quantise_h(0)
-        nc.vector.tensor_copy(out=early_cols[:], in_=early_t[:, 0 : E * PACK])
         layer(0)
         copy_out(1)
         sigma_done, mu_done = 0, 0
@@ -302,14 +296,14 @@ def tile_ensembleenvprob_pa_t_kernel(
                 quantise_h(r + 1)
             if r < NIT:
                 swish(r)
-            if r == NIT:
-                for k in range(EARLY):
-                    sigma_square(k)
             if r >= HEADS_FROM:
                 for step in range(1 if r < NIT else 4):
                     sigma_head(sigma_done, 2 * ((r + 1) % 2) + 1 if r < NIT else 4 + sigma_done % 4)
                     if r >= NIT:
                         sigma_square(sigma_done)
+                    if sigma_done == EARLY:
+                        for k in range(EARLY):
+                            sigma_square(k)
                     sigma_done += 1
                 for step in range(1 if r + 1 < NIT else 2 if r <= NIT else 0):
                     mu_head(mu_done, bank_no=2 * ((mu_done + 1) % 2) if r < NIT else mu_done % 4)

@@ -22,12 +22,9 @@ COLS = SL * P
 NIT = CH * E
 WEIGHT_SETS = 2 * E
 AHEAD = 2
-IO_SLOTS = 6
+IO_SLOTS = 7
 WEIGHT_SLOTS = 3
 WORK_BUFS = 3
-GROUP = CH // 2
-HEADS_FROM = GROUP * E
-EARLY = NIT - HEADS_FROM
 SCALAR_ONLY = 2 * WEIGHT_SETS
 BOUND_ROW = E
 LOG2_E = 1.0 / math.log(2.0)
@@ -43,7 +40,6 @@ def tile_ensembleenvprob_pa_t_kernel(
         const = ctx.enter_context(tc.tile_pool(name="const", bufs=1))
         keep = ctx.enter_context(tc.tile_pool(name="keep", bufs=1))
         io = ctx.enter_context(tc.tile_pool(name="io", bufs=IO_SLOTS))
-        early_out = ctx.enter_context(tc.tile_pool(name="early_out", bufs=2))
         weights = ctx.enter_context(tc.tile_pool(name="weights", bufs=WEIGHT_SLOTS))
         work = ctx.enter_context(tc.tile_pool(name="work", bufs=WORK_BUFS))
         psum = ctx.enter_context(tc.psum_pool(name="psum", bufs=1))
@@ -93,12 +89,7 @@ def tile_ensembleenvprob_pa_t_kernel(
         g_codes, g_scales, sigma_t, state, reward = {}, {}, {}, {}, {}
 
         def member_chunk(i):
-            half, rest = divmod(i, GROUP * E)
-            return rest // GROUP, half * GROUP + rest % GROUP
-
-        def iteration(k):
-            c, e = divmod(k, E)
-            return (c // GROUP) * GROUP * E + e * GROUP + c % GROUP
+            return i // CH, i % CH
 
         def load_h(i):
             e, c = member_chunk(i)
@@ -209,10 +200,10 @@ def tile_ensembleenvprob_pa_t_kernel(
                 out=g_codes[i][:].bitcast(FP8X4), scales=g_scales[i][:], in_=g_grouped[i][:]
             )
 
-        def mu_head(k, bank_no):
+        def mu_head(k):
             c, e = divmod(k, E)
-            i = iteration(k)
-            mu = bank(bank_no, [P, SL, OD])
+            i = e * CH + c
+            mu = bank(k % 4, [P, SL, OD])
             for t in range(SL):
                 nc.tensor.matmul_mx(
                     out=mu[:, t, :],
@@ -224,8 +215,7 @@ def tile_ensembleenvprob_pa_t_kernel(
                     stop=True,
                 )
             if e == 0:
-                pool, tag = (early_out, "early_out") if k < EARLY else (io, "io")
-                state[("mu", c)] = pool.tile([P, SL, E * SD], F32, name="ds_mu", tag=tag)
+                state[("mu", c)] = io.tile([P, SL, E * SD], F32, name="ds_mu", tag="io")
                 reward[("mu", c)] = work.tile([P, SL, E, RD], F32, name="r_mu", tag="reward", bufs=CH)
             bias = bmu_all[:, e * OD : (e + 1) * OD].unsqueeze(1)
             nc.vector.tensor_tensor(
@@ -242,9 +232,10 @@ def tile_ensembleenvprob_pa_t_kernel(
                     out=r_mu_view[c], in_=reward[("mu", c)][:].rearrange("p t e o -> p (t e o)")
                 )
 
-        def sigma_head(k, bank_no):
-            e, i = k % E, iteration(k)
-            raw = bank(bank_no, [P, COLS])
+        def sigma_head(k):
+            c, e = divmod(k, E)
+            i = e * CH + c
+            raw = bank(4 + k % 4, [P, COLS])
             nc.tensor.matmul_mx(
                 out=raw[:],
                 lhsT=head_codes[:, e, OD : 2 * OD].bitcast(FP8X4),
@@ -296,18 +287,13 @@ def tile_ensembleenvprob_pa_t_kernel(
                 quantise_h(r + 1)
             if r < NIT:
                 swish(r)
-            if r >= HEADS_FROM:
-                for step in range(1 if r < NIT else 4):
-                    sigma_head(sigma_done, 2 * ((r + 1) % 2) + 1 if r < NIT else 4 + sigma_done % 4)
-                    if r >= NIT:
-                        sigma_square(sigma_done)
-                    if sigma_done == EARLY:
-                        for k in range(EARLY):
-                            sigma_square(k)
-                    sigma_done += 1
-                for step in range(1 if r + 1 < NIT else 2 if r <= NIT else 0):
-                    mu_head(mu_done, bank_no=2 * ((mu_done + 1) % 2) if r < NIT else mu_done % 4)
-                    mu_done += 1
+            for step in range(4 if r >= NIT else 0):
+                sigma_head(sigma_done)
+                sigma_square(sigma_done)
+                sigma_done += 1
+            for step in range(2 if NIT - 1 <= r <= NIT else 0):
+                mu_head(mu_done)
+                mu_done += 1
             if r + 1 < NIT:
                 layer(r + 1)
             if 1 <= r <= NIT:
@@ -321,13 +307,13 @@ def tile_ensembleenvprob_pa_t_kernel(
                     quantise_weights(r // 2 + 1)
             if 1 <= r <= NIT:
                 quantise_g(r - 1)
-            if r == WEIGHT_SETS:
+            if r == 2 * WEIGHT_SETS:
                 nc.sync.dma_start(out=bmu_bf[:], in_=bmu.rearrange("e o -> (e o)").partition_broadcast(P))
                 nc.sync.dma_start(out=late[0:E, :], in_=bsig)
                 bounds = ((max_lv_s, 0, SD), (min_lv_s, 0, SD), (max_lv_r, SD, OD), (min_lv_r, SD, OD))
                 for k, (bound, start, stop) in enumerate(bounds):
                     nc.sync.dma_start(out=late[BOUND_ROW + k : BOUND_ROW + k + 1, start:stop], in_=bound)
-            if r == HEADS_FROM - 1:
+            if r == NIT - AHEAD:
                 nc.vector.tensor_copy(out=bmu_all[:], in_=bmu_bf[:])
                 late_t = bank(2 * ((r + 1) % 2), [P, P], BF16)
                 nc.tensor.transpose(late_t[:], late[:], ident_b[:])
@@ -377,12 +363,12 @@ def tile_ensembleenvprob_pa_t_kernel(
                     out=r_sg_view[c], in_=reward[("sg", c)][:].rearrange("p t e o -> p (t e o)")
                 )
 
-        for k in range(sigma_done, NIT):
-            sigma_head(k, 4 + k % 4)
-            sigma_square(k)
-        for k in range(NIT):
-            for step in range(4 if k == 0 else k % 2):
-                if mu_done < NIT:
-                    mu_head(mu_done, bank_no=mu_done % 4)
-                    mu_done += 1
-            sigma_out(k)
+        for k in range(sigma_done, 2 * NIT):
+            if k < NIT:
+                sigma_head(k)
+                sigma_square(k)
+            else:
+                sigma_out(k - NIT)
+            if k % 4 < 3 and mu_done < NIT:
+                mu_head(mu_done)
+                mu_done += 1

@@ -22,9 +22,13 @@ COLS = SL * P
 NIT = CH * E
 WEIGHT_SETS = 2 * E
 AHEAD = 2
-IO_SLOTS = 7
+H_SLOTS = 7
+OUT_SLOTS = 6
 WEIGHT_SLOTS = 3
 WORK_BUFS = 3
+HALVES = 2
+GROUP = CH // HALVES
+HIT = GROUP * E
 SCALAR_ONLY = 2 * WEIGHT_SETS
 BOUND_ROW = E
 LOG2_E = 1.0 / math.log(2.0)
@@ -39,7 +43,8 @@ def tile_ensembleenvprob_pa_t_kernel(
     with ExitStack() as ctx:
         const = ctx.enter_context(tc.tile_pool(name="const", bufs=1))
         keep = ctx.enter_context(tc.tile_pool(name="keep", bufs=1))
-        io = ctx.enter_context(tc.tile_pool(name="io", bufs=IO_SLOTS))
+        h_in = ctx.enter_context(tc.tile_pool(name="h_in", bufs=H_SLOTS))
+        outs = ctx.enter_context(tc.tile_pool(name="outs", bufs=OUT_SLOTS))
         weights = ctx.enter_context(tc.tile_pool(name="weights", bufs=WEIGHT_SLOTS))
         work = ctx.enter_context(tc.tile_pool(name="work", bufs=WORK_BUFS))
         psum = ctx.enter_context(tc.psum_pool(name="psum", bufs=1))
@@ -86,14 +91,20 @@ def tile_ensembleenvprob_pa_t_kernel(
 
         h_sb, w_raw, w_grouped = {}, {}, {}
         xt, h_grouped, h_codes, h_scales, acc, g_planes, g_grouped = {}, {}, {}, {}, {}, {}, {}
+        mu_done = []
         g_codes, g_scales, sigma_t, state, reward = {}, {}, {}, {}, {}
 
         def member_chunk(i):
-            return i // CH, i % CH
+            half, rest = divmod(i, HIT)
+            return rest // GROUP, half * GROUP + rest % GROUP
+
+        def iteration(k):
+            c, e = divmod(k, E)
+            return (c // GROUP) * HIT + e * GROUP + c % GROUP
 
         def load_h(i):
             e, c = member_chunk(i)
-            h_sb[i] = io.tile([P, SL, HID], BF16, name="h_sb", tag="io")
+            h_sb[i] = h_in.tile([P, SL, HID], BF16, name="h_sb", tag="h_sb")
             pieces = 2 if i == 0 else 1
             step = SL // pieces
             for s in range(pieces):
@@ -145,15 +156,15 @@ def tile_ensembleenvprob_pa_t_kernel(
                         words[:, base + u * P : base + (u + 1) * P],
                         ident_f[:],
                     )
-            if half == 1 and i + IO_SLOTS < NIT:
-                load_h(i + IO_SLOTS)
+            if half == 1 and i + H_SLOTS < NIT:
+                load_h(i + H_SLOTS)
 
         def copy_out(i):
             h_grouped[i] = work.tile([P, 2 * HID], F32, name="h_grouped", tag="h_grouped", align_bytes=64)
             for half in range(2):
                 dst = h_grouped[i][:, half * HID : (half + 1) * HID].rearrange("p (n u) -> p n u", u=2)
                 src = xt[(i, half)][:].rearrange("p u n -> p n u")
-                on_scalar = i != 1 and (half == 0 or i < SCALAR_ONLY)
+                on_scalar = i not in (2, HIT + 2, HIT + 3) and (half == 0 or 0 < i < SCALAR_ONLY)
                 if on_scalar:
                     nc.scalar.copy(out=dst, in_=src)
                 else:
@@ -201,8 +212,9 @@ def tile_ensembleenvprob_pa_t_kernel(
             )
 
         def mu_head(k):
+            mu_done.append(k)
             c, e = divmod(k, E)
-            i = e * CH + c
+            i = iteration(k)
             mu = bank(k % 4, [P, SL, OD])
             for t in range(SL):
                 nc.tensor.matmul_mx(
@@ -215,7 +227,7 @@ def tile_ensembleenvprob_pa_t_kernel(
                     stop=True,
                 )
             if e == 0:
-                state[("mu", c)] = io.tile([P, SL, E * SD], F32, name="ds_mu", tag="io")
+                state[("mu", c)] = outs.tile([P, SL, E * SD], F32, name="ds_mu", tag="out")
                 reward[("mu", c)] = work.tile([P, SL, E, RD], F32, name="r_mu", tag="reward", bufs=CH)
             bias = bmu_all[:, e * OD : (e + 1) * OD].unsqueeze(1)
             nc.vector.tensor_tensor(
@@ -233,8 +245,7 @@ def tile_ensembleenvprob_pa_t_kernel(
                 )
 
         def sigma_head(k):
-            c, e = divmod(k, E)
-            i = e * CH + c
+            e, i = k % E, iteration(k)
             raw = bank(4 + k % 4, [P, COLS])
             nc.tensor.matmul_mx(
                 out=raw[:],
@@ -245,7 +256,7 @@ def tile_ensembleenvprob_pa_t_kernel(
                 start=True,
                 stop=True,
             )
-            sigma_t[k] = keep.tile([P, COLS], F32, name="sg%d" % k)
+            sigma_t[k] = keep.tile([P, COLS], F32, name="sg", tag="sg%d" % (k % HIT))
             nc.scalar.activation(
                 out=sigma_t[k][:], in_=raw[:], func=ACT.Tanh, bias=sig_bias[:, e : e + 1], scale=1.0
             )
@@ -256,87 +267,6 @@ def tile_ensembleenvprob_pa_t_kernel(
                 op0=ALU.mult, op1=ALU.add,
             )
 
-        load_weights(0)
-        load_h(0)
-        nc.sync.dma_start(out=early[0 : E * PACK, :], in_=bh.rearrange("e (j p) -> (e j) p", p=P))
-        load_h(1)
-        load_weights(1)
-        load_h(2)
-        load_weights(2)
-        for i in range(3, IO_SLOTS):
-            load_h(i)
-        regroup_weights(0)
-        transposes(0, 0)
-        transposes(0, 1)
-        early_t = bank(7, [P, P], BF16)
-        nc.tensor.transpose(early_t[:], early[:], ident_b[:])
-        quantise_weights(0)
-        nc.vector.tensor_copy(out=early_cols[:], in_=early_t[:, 0 : E * PACK])
-        copy_out(0)
-        transposes(1, 0)
-        transposes(1, 1)
-        quantise_h(0)
-        layer(0)
-        copy_out(1)
-        sigma_done, mu_done = 0, 0
-        for r in range(NIT + 2):
-            if r + AHEAD < NIT:
-                transposes(r + AHEAD, 0)
-                transposes(r + AHEAD, 1)
-            if r + 1 < NIT:
-                quantise_h(r + 1)
-            if r < NIT:
-                swish(r)
-            for step in range(4 if r >= NIT else 0):
-                sigma_head(sigma_done)
-                sigma_square(sigma_done)
-                sigma_done += 1
-            for step in range(2 if NIT - 1 <= r <= NIT else 0):
-                mu_head(mu_done)
-                mu_done += 1
-            if r + 1 < NIT:
-                layer(r + 1)
-            if 1 <= r <= NIT:
-                regroup_g(r - 1)
-            if r + AHEAD < NIT:
-                copy_out(r + AHEAD)
-            if r // 2 + 1 < WEIGHT_SETS:
-                if r % 2 == 0:
-                    regroup_weights(r // 2 + 1)
-                else:
-                    quantise_weights(r // 2 + 1)
-            if 1 <= r <= NIT:
-                quantise_g(r - 1)
-            if r == 2 * WEIGHT_SETS:
-                nc.sync.dma_start(out=bmu_bf[:], in_=bmu.rearrange("e o -> (e o)").partition_broadcast(P))
-                nc.sync.dma_start(out=late[0:E, :], in_=bsig)
-                bounds = ((max_lv_s, 0, SD), (min_lv_s, 0, SD), (max_lv_r, SD, OD), (min_lv_r, SD, OD))
-                for k, (bound, start, stop) in enumerate(bounds):
-                    nc.sync.dma_start(out=late[BOUND_ROW + k : BOUND_ROW + k + 1, start:stop], in_=bound)
-            if r == NIT - AHEAD:
-                nc.vector.tensor_copy(out=bmu_all[:], in_=bmu_bf[:])
-                late_t = bank(2 * ((r + 1) % 2), [P, P], BF16)
-                nc.tensor.transpose(late_t[:], late[:], ident_b[:])
-                nc.vector.tensor_copy(out=late_cols[:], in_=late_t[:, 0 : BOUND_ROW + 4])
-                nc.vector.tensor_tensor(
-                    out=hi_lo[:], in0=late_cols[:, BOUND_ROW : BOUND_ROW + 2],
-                    in1=late_cols[:, BOUND_ROW + 2 : BOUND_ROW + 4], op=ALU.add,
-                )
-                nc.gpsimd.tensor_scalar(
-                    out=half_hi[:], in0=hi_lo[:, 0:1], scalar1=0.5, scalar2=0.0, op0=ALU.mult, op1=ALU.add
-                )
-                nc.vector.tensor_scalar(
-                    out=sig_bias[:], in0=late_cols[:, 0:E], scalar1=half_hi[:], scalar2=None, op0=ALU.subtract
-                )
-                nc.gpsimd.tensor_scalar(
-                    out=log2_hi_lo[:], in0=hi_lo[:], scalar1=LOG2_E, scalar2=0.0, op0=ALU.mult, op1=ALU.add
-                )
-                nc.gpsimd.tensor_tensor(out=exp_hi_lo[:], in0=twos[:], in1=log2_hi_lo[:], op=ALU.pow)
-                nc.gpsimd.tensor_scalar(
-                    out=slope[:], in0=exp_hi_lo[:, 0:1], scalar1=0.5, scalar2=0.0, op0=ALU.mult, op1=ALU.add
-                )
-                nc.gpsimd.tensor_tensor(out=offset[:], in0=slope[:], in1=exp_hi_lo[:, 1:2], op=ALU.add)
-
         def sigma_out(k):
             c, e = divmod(k, E)
             back = bank(4 + k % 4, [P, SL, OD])
@@ -346,7 +276,7 @@ def tile_ensembleenvprob_pa_t_kernel(
             if c == CH - 1:
                 first, members = (0, E - 1) if e < E - 1 else (E - 1, 1)
             if e == first:
-                state[("sg", c)] = io.tile([P, SL, members * SD], F32, name="ds_sg", tag="io")
+                state[("sg", c)] = outs.tile([P, SL, members * SD], F32, name="ds_sg", tag="out")
             if e == 0:
                 reward[("sg", c)] = work.tile([P, SL, E, RD], F32, name="r_sg", tag="reward", bufs=CH)
             nc.scalar.activation(
@@ -363,12 +293,105 @@ def tile_ensembleenvprob_pa_t_kernel(
                     out=r_sg_view[c], in_=reward[("sg", c)][:].rearrange("p t e o -> p (t e o)")
                 )
 
-        for k in range(sigma_done, 2 * NIT):
-            if k < NIT:
+        def prepare_bounds(bank_no):
+            nc.vector.tensor_copy(out=bmu_all[:], in_=bmu_bf[:])
+            late_t = bank(bank_no, [P, P], BF16)
+            nc.tensor.transpose(late_t[:], late[:], ident_b[:])
+            nc.vector.tensor_copy(out=late_cols[:], in_=late_t[:, 0 : BOUND_ROW + 4])
+            nc.vector.tensor_tensor(
+                out=hi_lo[:], in0=late_cols[:, BOUND_ROW : BOUND_ROW + 2],
+                in1=late_cols[:, BOUND_ROW + 2 : BOUND_ROW + 4], op=ALU.add,
+            )
+            nc.gpsimd.tensor_scalar(
+                out=half_hi[:], in0=hi_lo[:, 0:1], scalar1=0.5, scalar2=0.0, op0=ALU.mult, op1=ALU.add
+            )
+            nc.vector.tensor_scalar(
+                out=sig_bias[:], in0=late_cols[:, 0:E], scalar1=half_hi[:], scalar2=None, op0=ALU.subtract
+            )
+            nc.gpsimd.tensor_scalar(
+                out=log2_hi_lo[:], in0=hi_lo[:], scalar1=LOG2_E, scalar2=0.0, op0=ALU.mult, op1=ALU.add
+            )
+            nc.gpsimd.tensor_tensor(out=exp_hi_lo[:], in0=twos[:], in1=log2_hi_lo[:], op=ALU.pow)
+            nc.gpsimd.tensor_scalar(
+                out=slope[:], in0=exp_hi_lo[:, 0:1], scalar1=0.5, scalar2=0.0, op0=ALU.mult, op1=ALU.add
+            )
+            nc.gpsimd.tensor_tensor(out=offset[:], in0=slope[:], in1=exp_hi_lo[:, 1:2], op=ALU.add)
+
+        def heads(half):
+            first = half * HIT
+            regroup_g(first + HIT - 1)
+            for k in range(first, first + 4):
                 sigma_head(k)
                 sigma_square(k)
-            else:
-                sigma_out(k - NIT)
-            if k % 4 < 3 and mu_done < NIT:
-                mu_head(mu_done)
-                mu_done += 1
+            for step in range(4):
+                mu_head(len(mu_done))
+                if step == 0:
+                    quantise_g(first + HIT - 1)
+            for k in range(first + 4, first + HIT):
+                if k >= first + 10:
+                    mu_head(len(mu_done))
+                sigma_head(k)
+                sigma_square(k)
+            for k in range(first, first + HIT):
+                if len(mu_done) < first + HIT:
+                    mu_head(len(mu_done))
+                sigma_out(k)
+
+        load_weights(0)
+        load_h(0)
+        nc.sync.dma_start(out=early[0 : E * PACK, :], in_=bh.rearrange("e (j p) -> (e j) p", p=P))
+        load_h(1)
+        load_weights(1)
+        load_h(2)
+        load_weights(2)
+        for i in range(3, H_SLOTS):
+            load_h(i)
+        regroup_weights(0)
+        transposes(0, 0)
+        transposes(0, 1)
+        early_t = bank(7, [P, P], BF16)
+        nc.tensor.transpose(early_t[:], early[:], ident_b[:])
+        quantise_weights(0)
+        nc.vector.tensor_copy(out=early_cols[:], in_=early_t[:, 0 : E * PACK])
+        copy_out(0)
+        transposes(1, 0)
+        transposes(1, 1)
+        quantise_h(0)
+        copy_out(1)
+        layer(0)
+        for r in range(NIT):
+            half, place = divmod(r, HIT)
+            if r + AHEAD < NIT:
+                transposes(r + AHEAD, 0)
+                transposes(r + AHEAD, 1)
+            if r + 1 < NIT:
+                quantise_h(r + 1)
+            swish(r)
+            if r + AHEAD >= NIT:
+                for step in range(1 if r + 1 < NIT else 2):
+                    mu_head(len(mu_done))
+            if place + 1 < HIT:
+                layer(r + 1)
+            if place > 0:
+                regroup_g(r - 1)
+            if r // 2 + 1 < WEIGHT_SETS:
+                if r % 2 == 0:
+                    regroup_weights(r // 2 + 1)
+                else:
+                    quantise_weights(r // 2 + 1)
+            if r + AHEAD < NIT:
+                copy_out(r + AHEAD)
+            if place > 0:
+                quantise_g(r - 1)
+            if r == WEIGHT_SETS:
+                nc.sync.dma_start(out=bmu_bf[:], in_=bmu.rearrange("e o -> (e o)").partition_broadcast(P))
+                nc.sync.dma_start(out=late[0:E, :], in_=bsig)
+                bounds = ((max_lv_s, 0, SD), (min_lv_s, 0, SD), (max_lv_r, SD, OD), (min_lv_r, SD, OD))
+                for k, (bound, start, stop) in enumerate(bounds):
+                    nc.sync.dma_start(out=late[BOUND_ROW + k : BOUND_ROW + k + 1, start:stop], in_=bound)
+            if r == HIT - 3:
+                prepare_bounds(2 * ((r + 1) % 2))
+            if place + 1 == HIT:
+                heads(half)
+                if r + 1 < NIT:
+                    layer(r + 1)

@@ -164,7 +164,7 @@ def tile_ensembleenvprob_pa_t_kernel(
             for half in range(2):
                 dst = h_grouped[i][:, half * HID : (half + 1) * HID].rearrange("p (n u) -> p n u", u=2)
                 src = xt[(i, half)][:].rearrange("p u n -> p n u")
-                on_scalar = i not in (2, HIT + 2, HIT + 3) and (half == 0 or 0 < i < SCALAR_ONLY)
+                on_scalar = i != 2 and not HIT <= i < HIT + 4 and (half == 0 or 0 < i < SCALAR_ONLY)
                 if on_scalar:
                     nc.scalar.copy(out=dst, in_=src)
                 else:
@@ -294,7 +294,6 @@ def tile_ensembleenvprob_pa_t_kernel(
                 )
 
         def prepare_bounds(bank_no):
-            nc.vector.tensor_copy(out=bmu_all[:], in_=bmu_bf[:])
             late_t = bank(bank_no, [P, P], BF16)
             nc.tensor.transpose(late_t[:], late[:], ident_b[:])
             nc.vector.tensor_copy(out=late_cols[:], in_=late_t[:, 0 : BOUND_ROW + 4])
@@ -304,9 +303,6 @@ def tile_ensembleenvprob_pa_t_kernel(
             )
             nc.gpsimd.tensor_scalar(
                 out=half_hi[:], in0=hi_lo[:, 0:1], scalar1=0.5, scalar2=0.0, op0=ALU.mult, op1=ALU.add
-            )
-            nc.vector.tensor_scalar(
-                out=sig_bias[:], in0=late_cols[:, 0:E], scalar1=half_hi[:], scalar2=None, op0=ALU.subtract
             )
             nc.gpsimd.tensor_scalar(
                 out=log2_hi_lo[:], in0=hi_lo[:], scalar1=LOG2_E, scalar2=0.0, op0=ALU.mult, op1=ALU.add
@@ -320,22 +316,41 @@ def tile_ensembleenvprob_pa_t_kernel(
         def heads(half):
             first = half * HIT
             regroup_g(first + HIT - 1)
-            for k in range(first, first + 4):
-                sigma_head(k)
-                sigma_square(k)
-            for step in range(4):
-                mu_head(len(mu_done))
-                if step == 0:
-                    quantise_g(first + HIT - 1)
-            for k in range(first + 4, first + HIT):
-                if k >= first + 10:
+            following = first + HIT
+            if following < NIT:
+                copy_out(following)
+                quantise_g(following - 1)
+                copy_out(following + 1)
+                quantise_h(following)
+                for k in range(first, following):
+                    sigma_head(k)
+                    sigma_square(k)
+                for step in range(4):
                     mu_head(len(mu_done))
-                sigma_head(k)
-                sigma_square(k)
-            for k in range(first, first + HIT):
-                if len(mu_done) < first + HIT:
+            else:
+                for k in range(first, first + 4):
+                    sigma_head(k)
+                    sigma_square(k)
+                for step in range(4):
+                    mu_head(len(mu_done))
+                    if step == 0:
+                        quantise_g(following - 1)
+                for k in range(first + 4, following):
+                    if k >= first + 10:
+                        mu_head(len(mu_done))
+                    sigma_head(k)
+                    sigma_square(k)
+            for k in range(first, following):
+                if len(mu_done) < following:
                     mu_head(len(mu_done))
                 sigma_out(k)
+            if following < NIT:
+                quantise_h(following + 1)
+                for i in (following + 2, following + 3):
+                    transposes(i, 0)
+                    transposes(i, 1)
+                    copy_out(i)
+                layer(following)
 
         load_weights(0)
         load_h(0)
@@ -349,37 +364,41 @@ def tile_ensembleenvprob_pa_t_kernel(
         regroup_weights(0)
         transposes(0, 0)
         transposes(0, 1)
-        early_t = bank(7, [P, P], BF16)
-        nc.tensor.transpose(early_t[:], early[:], ident_b[:])
         quantise_weights(0)
-        nc.vector.tensor_copy(out=early_cols[:], in_=early_t[:, 0 : E * PACK])
         copy_out(0)
         transposes(1, 0)
         transposes(1, 1)
+        early_t = bank(7, [P, P], BF16)
+        nc.tensor.transpose(early_t[:], early[:], ident_b[:])
         quantise_h(0)
+        nc.vector.tensor_copy(out=early_cols[:], in_=early_t[:, 0 : E * PACK])
         copy_out(1)
         layer(0)
         for r in range(NIT):
             half, place = divmod(r, HIT)
-            if r + AHEAD < NIT:
+            if r + AHEAD < NIT and (half == 0 or place + AHEAD >= 4):
                 transposes(r + AHEAD, 0)
                 transposes(r + AHEAD, 1)
-            if r + 1 < NIT:
+            if place + 1 < HIT and (half == 0 or place > 0):
                 quantise_h(r + 1)
+            if r == HIT - 3:
+                prepare_bounds(2 * ((r + 1) % 2))
             swish(r)
-            if r + AHEAD >= NIT:
-                for step in range(1 if r + 1 < NIT else 2):
-                    mu_head(len(mu_done))
+            if r + AHEAD == NIT:
+                mu_head(len(mu_done))
             if place + 1 < HIT:
                 layer(r + 1)
             if place > 0:
                 regroup_g(r - 1)
+            if r + 1 == NIT:
+                mu_head(len(mu_done))
+                mu_head(len(mu_done))
             if r // 2 + 1 < WEIGHT_SETS:
                 if r % 2 == 0:
                     regroup_weights(r // 2 + 1)
                 else:
                     quantise_weights(r // 2 + 1)
-            if r + AHEAD < NIT:
+            if place + AHEAD < HIT and (half == 0 or place + AHEAD >= 4):
                 copy_out(r + AHEAD)
             if place > 0:
                 quantise_g(r - 1)
@@ -390,8 +409,9 @@ def tile_ensembleenvprob_pa_t_kernel(
                 for k, (bound, start, stop) in enumerate(bounds):
                     nc.sync.dma_start(out=late[BOUND_ROW + k : BOUND_ROW + k + 1, start:stop], in_=bound)
             if r == HIT - 3:
-                prepare_bounds(2 * ((r + 1) % 2))
+                nc.vector.tensor_copy(out=bmu_all[:], in_=bmu_bf[:])
+                nc.vector.tensor_scalar(
+                    out=sig_bias[:], in0=late_cols[:, 0:E], scalar1=half_hi[:], scalar2=None, op0=ALU.subtract
+                )
             if place + 1 == HIT:
                 heads(half)
-                if r + 1 < NIT:
-                    layer(r + 1)

@@ -29,7 +29,6 @@ WORK_BUFS = 3
 HALVES = 2
 GROUP = CH // HALVES
 HIT = GROUP * E
-SCALAR_ONLY = 2 * WEIGHT_SETS
 BOUND_ROW = E
 LOG2_E = 1.0 / math.log(2.0)
 FLOPS = 2 * N * E * HID * (HID + 2 * OD)
@@ -164,7 +163,7 @@ def tile_ensembleenvprob_pa_t_kernel(
             for half in range(2):
                 dst = h_grouped[i][:, half * HID : (half + 1) * HID].rearrange("p (n u) -> p n u", u=2)
                 src = xt[(i, half)][:].rearrange("p u n -> p n u")
-                on_scalar = i != 2 and not HIT <= i < HIT + 4 and (half == 0 or 0 < i < SCALAR_ONLY)
+                on_scalar = i != 2 and not HIT <= i < HIT + 6 and (half == 0 or 0 < i < HIT and i % 4 != 2 or i >= NIT - 2)
                 if on_scalar:
                     nc.scalar.copy(out=dst, in_=src)
                 else:
@@ -351,6 +350,11 @@ def tile_ensembleenvprob_pa_t_kernel(
                     transposes(i, 1)
                     copy_out(i)
                 layer(following)
+                quantise_h(following + 2)
+                for i in (following + 4, following + 5):
+                    transposes(i, 0)
+                    transposes(i, 1)
+                    copy_out(i)
 
         load_weights(0)
         load_h(0)
@@ -376,10 +380,10 @@ def tile_ensembleenvprob_pa_t_kernel(
         layer(0)
         for r in range(NIT):
             half, place = divmod(r, HIT)
-            if r + AHEAD < NIT and (half == 0 or place + AHEAD >= 4):
+            if r + AHEAD < NIT and (half == 0 or place + AHEAD >= 6):
                 transposes(r + AHEAD, 0)
                 transposes(r + AHEAD, 1)
-            if place + 1 < HIT and (half == 0 or place > 0):
+            if place + 1 < HIT and (half == 0 or place > 1):
                 quantise_h(r + 1)
             if r == HIT - 3:
                 prepare_bounds(2 * ((r + 1) % 2))
@@ -398,7 +402,7 @@ def tile_ensembleenvprob_pa_t_kernel(
                     regroup_weights(r // 2 + 1)
                 else:
                     quantise_weights(r // 2 + 1)
-            if place + AHEAD < HIT and (half == 0 or place + AHEAD >= 4):
+            if place + AHEAD < HIT and (half == 0 or place + AHEAD >= 6):
                 copy_out(r + AHEAD)
             if place > 0:
                 quantise_g(r - 1)

import math
from contextlib import ExitStack

import concourse.mybir as mybir
from concourse.masks import make_identity

F32 = mybir.dt.float32
BF16 = mybir.dt.bfloat16
U32 = mybir.dt.uint32
U8 = mybir.dt.uint8
FP8X4 = mybir.dt.float8_e4m3fn_x4
ACT = mybir.ActivationFunctionType
ALU = mybir.AluOpType

N, E, HID, OD, SD = 4096, 3, 512, 128, 120
RD = OD - SD
P = 128
PACK = 4
CH = 8
SL = N // (CH * P)
COLS = SL * P
NIT = CH * E
WEIGHT_SETS = 2 * E
AHEAD = 2
H_SLOTS = 7
OUT_SLOTS = 6
WEIGHT_SLOTS = 3
WORK_BUFS = 3
HALVES = 2
GROUP = CH // HALVES
HIT = GROUP * E
BOUND_ROW = E
LOG2_E = 1.0 / math.log(2.0)
FLOPS = 2 * N * E * HID * (HID + 2 * OD)


def tile_ensembleenvprob_pa_t_kernel(
    tc, h, Wh, bh, Wmu, bmu, Wsig, bsig, max_lv_s, min_lv_s, max_lv_r, min_lv_r,
    out_0, out_1, out_2, out_3,
):
    nc = tc.nc
    with ExitStack() as ctx:
        const = ctx.enter_context(tc.tile_pool(name="const", bufs=1))
        keep = ctx.enter_context(tc.tile_pool(name="keep", bufs=1))
        h_in = ctx.enter_context(tc.tile_pool(name="h_in", bufs=H_SLOTS))
        outs = ctx.enter_context(tc.tile_pool(name="outs", bufs=OUT_SLOTS))
        weights = ctx.enter_context(tc.tile_pool(name="weights", bufs=WEIGHT_SLOTS))
        work = ctx.enter_context(tc.tile_pool(name="work", bufs=WORK_BUFS))
        psum = ctx.enter_context(tc.psum_pool(name="psum", bufs=1))
        ctx.enter_context(tc.manual_schedule())

        h_view = h.rearrange("(p c t) e k -> c e p t k", c=CH, t=SL)
        ds_mu_view = out_0.rearrange("(p c t) e o -> c p t (e o)", c=CH, t=SL)
        ds_sg_view = out_1.rearrange("(p c t) e o -> c p t (e o)", c=CH, t=SL)
        r_mu_view = out_2.rearrange("(p c t) e o -> c p (t e o)", c=CH, t=SL)
        r_sg_view = out_3.rearrange("(p c t) e o -> c p (t e o)", c=CH, t=SL)

        def bank(k, shape, dtype=F32):
            return psum.tile(shape, dtype, name="bank", tag="bank%d" % k)

        ident_f = const.tile([P, P], F32, name="ident_f")
        make_identity(nc, ident_f[:])
        ident_b = const.tile([P, P], BF16, name="ident_b")
        make_identity(nc, ident_b[:])
        early = const.tile([P, P], BF16, name="early")
        nc.vector.memset(early[:], 0.0)
        warm = const.tile([P, 1], F32, name="warm")
        nc.vector.memset(warm[:], 0.0)
        nc.scalar.activation(out=warm[:], in_=warm[:], func=ACT.Silu)
        late = const.tile([P, P], BF16, name="late")
        nc.gpsimd.memset(late[:], 0.0)
        twos = const.tile([P, 2], F32, name="twos")
        nc.gpsimd.memset(twos[:], 2.0)

        wh_codes = const.tile([P, E, HID], U32, name="wh_codes", align_bytes=64)
        wh_scales = const.tile([P, E, HID], U8, name="wh_scales", align_bytes=64)
        head_codes = const.tile([P, E, 2 * OD], U32, name="head_codes", align_bytes=64)
        head_scales = const.tile([P, E, 2 * OD], U8, name="head_scales", align_bytes=64)
        bmu_bf = const.tile([P, E * OD], BF16, name="bmu_bf")
        bmu_all = const.tile([P, E * OD], F32, name="bmu_all")
        early_cols = const.tile([P, E * PACK], F32, name="early_cols")
        late_cols = const.tile([P, BOUND_ROW + 4], F32, name="late_cols")
        hi_lo = const.tile([P, 2], F32, name="hi_lo")
        log2_hi_lo = const.tile([P, 2], F32, name="log2_hi_lo")
        exp_hi_lo = const.tile([P, 2], F32, name="exp_hi_lo")
        half_hi = const.tile([P, 1], F32, name="half_hi")
        sig_bias = const.tile([P, E], F32, name="sig_bias")
        slope = const.tile([P, 1], F32, name="slope")
        offset = const.tile([P, 1], F32, name="offset")

        h_sb, w_raw, w_grouped = {}, {}, {}
        xt, h_grouped, h_codes, h_scales, acc, g_planes, g_grouped = {}, {}, {}, {}, {}, {}, {}
        mu_done = []
        g_codes, g_scales, sigma_t, state, reward = {}, {}, {}, {}, {}

        def member_chunk(i):
            half, rest = divmod(i, HIT)
            return rest // GROUP, half * GROUP + rest % GROUP

        def iteration(k):
            c, e = divmod(k, E)
            return (c // GROUP) * HIT + e * GROUP + c % GROUP

        def load_h(i):
            e, c = member_chunk(i)
            h_sb[i] = h_in.tile([P, SL, HID], BF16, name="h_sb", tag="h_sb")
            pieces = 2 if i == 0 else 1
            step = SL // pieces
            for s in range(pieces):
                rows = slice(s * step, (s + 1) * step)
                nc.sync.dma_start(out=h_sb[i][:, rows, :], in_=h_view[c, e][:, rows, :])

        def load_weights(w):
            if w < E:
                w_raw[w] = weights.tile([P, PACK, HID], BF16, name="w_raw", tag="w_raw")
                nc.sync.dma_start(
                    out=w_raw[w][:].rearrange("p (u a) f -> p u (a f)", u=2),
                    in_=Wh[w].rearrange("(u p a) f -> p u (a f)", u=2, a=2),
                )
            else:
                w_raw[w] = weights.tile([P, PACK, 2 * OD], BF16, name="w_raw", tag="w_raw")
                for m, head in enumerate((Wmu, Wsig)):
                    nc.sync.dma_start(
                        out=w_raw[w][:, :, m * OD : (m + 1) * OD],
                        in_=head[w - E].rearrange("(j p) o -> p j o", p=P),
                    )

        def regroup(dst, src):
            nc.vector.tensor_copy(
                out=dst.rearrange("p (c i t) -> p c t i", i=4, t=PACK),
                in_=src.rearrange("p t (c i) -> p c t i", i=4),
            )

        def regroup_weights(w):
            width = HID if w < E else 2 * OD
            w_grouped[w] = work.tile([P, PACK * width], BF16, name="w_grouped", tag="grouped", align_bytes=64)
            regroup(w_grouped[w][:], w_raw[w][:])
            if w + WEIGHT_SLOTS < WEIGHT_SETS:
                load_weights(w + WEIGHT_SLOTS)

        def quantise_weights(w):
            codes, scales = (wh_codes, wh_scales) if w < E else (head_codes, head_scales)
            nc.vector.quantize_mx(
                out=codes[:, w % E, :].bitcast(FP8X4), scales=scales[:, w % E, :], in_=w_grouped[w][:]
            )

        def transposes(i, half):
            words = h_sb[i][:].rearrange("p t k -> p (t k)").bitcast(F32)
            xt[(i, half)] = bank(2 * (i % 2) + half, [P, 2, 2 * P])
            for tt in range(2):
                base = (2 * half + tt) * (HID // 2)
                for u in range(2):
                    nc.tensor.transpose(
                        xt[(i, half)][:, u, tt * P : (tt + 1) * P],
                        words[:, base + u * P : base + (u + 1) * P],
                        ident_f[:],
                    )
            if half == 1 and i + H_SLOTS < NIT:
                load_h(i + H_SLOTS)

        def copy_out(i):
            h_grouped[i] = work.tile([P, 2 * HID], F32, name="h_grouped", tag="h_grouped", align_bytes=64)
            for half in range(2):
                dst = h_grouped[i][:, half * HID : (half + 1) * HID].rearrange("p (n u) -> p n u", u=2)
                src = xt[(i, half)][:].rearrange("p u n -> p n u")
                on_scalar = i != 2 and not HIT <= i < HIT + 6 and (half == 0 or 0 < i < HIT and i % 4 != 2 or i >= NIT - 2)
                if on_scalar:
                    nc.scalar.copy(out=dst, in_=src)
                else:
                    nc.vector.tensor_copy(out=dst, in_=src)

        def quantise_h(i):
            h_codes[i] = work.tile([P, COLS], U32, name="h_codes", tag="h_codes", align_bytes=64)
            h_scales[i] = work.tile([P, COLS], U8, name="h_scales", tag="h_scales", align_bytes=64)
            nc.vector.quantize_mx(
                out=h_codes[i][:].bitcast(FP8X4), scales=h_scales[i][:], in_=h_grouped[i][:].bitcast(BF16)
            )

        def layer(i):
            e = member_chunk(i)[0]
            for j in range(PACK):
                acc[(i, j)] = bank(4 + j, [P, COLS])
                nc.tensor.matmul_mx(
                    out=acc[(i, j)][:],
                    lhsT=wh_codes[:, e, j * P : (j + 1) * P].bitcast(FP8X4),
                    lhsT_scale=wh_scales[:, e, j * P : (j + 1) * P],
                    rhs=h_codes[i][:].bitcast(FP8X4),
                    rhs_scale=h_scales[i][:],
                    start=True,
                    stop=True,
                )

        def swish(i):
            e = member_chunk(i)[0]
            g_planes[i] = work.tile([P, PACK, COLS], BF16, name="g_planes", tag="g_planes")
            for j in range(PACK):
                nc.scalar.activation(
                    out=g_planes[i][:, j, :], in_=acc[(i, j)][:], func=ACT.Silu,
                    bias=early_cols[:, PACK * e + j : PACK * e + j + 1], scale=1.0,
                )

        def regroup_g(i):
            g_grouped[i] = work.tile([P, PACK * COLS], BF16, name="g_grouped", tag="grouped", align_bytes=64)
            regroup(g_grouped[i][:], g_planes[i][:])

        def quantise_g(i):
            g_codes[i] = keep.tile([P, COLS], U32, name="g_codes%d" % i, align_bytes=64)
            g_scales[i] = keep.tile([P, COLS], U8, name="g_scales%d" % i, align_bytes=64)
            nc.vector.quantize_mx(
                out=g_codes[i][:].bitcast(FP8X4), scales=g_scales[i][:], in_=g_grouped[i][:]
            )

        def mu_head(k):
            mu_done.append(k)
            c, e = divmod(k, E)
            i = iteration(k)
            mu = bank(k % 4, [P, SL, OD])
            for t in range(SL):
                nc.tensor.matmul_mx(
                    out=mu[:, t, :],
                    lhsT=g_codes[i][:, t * P : (t + 1) * P].bitcast(FP8X4),
                    lhsT_scale=g_scales[i][:, t * P : (t + 1) * P],
                    rhs=head_codes[:, e, 0:OD].bitcast(FP8X4),
                    rhs_scale=head_scales[:, e, 0:OD],
                    start=True,
                    stop=True,
                )
            if e == 0:
                state[("mu", c)] = outs.tile([P, SL, E * SD], F32, name="ds_mu", tag="out")
                reward[("mu", c)] = work.tile([P, SL, E, RD], F32, name="r_mu", tag="reward", bufs=CH)
            bias = bmu_all[:, e * OD : (e + 1) * OD].unsqueeze(1)
            nc.vector.tensor_tensor(
                out=state[("mu", c)][:, :, e * SD : (e + 1) * SD], in0=mu[:, :, 0:SD],
                in1=bias[:, :, 0:SD].to_broadcast([P, SL, SD]), op=ALU.add,
            )
            nc.vector.tensor_tensor(
                out=reward[("mu", c)][:, :, e, :], in0=mu[:, :, SD:OD],
                in1=bias[:, :, SD:OD].to_broadcast([P, SL, RD]), op=ALU.add,
            )
            if e == E - 1:
                nc.sync.dma_start(out=ds_mu_view[c], in_=state[("mu", c)][:])
                nc.sync.dma_start(
                    out=r_mu_view[c], in_=reward[("mu", c)][:].rearrange("p t e o -> p (t e o)")
                )

        def sigma_head(k):
            e, i = k % E, iteration(k)
            raw = bank(4 + k % 4, [P, COLS])
            nc.tensor.matmul_mx(
                out=raw[:],
                lhsT=head_codes[:, e, OD : 2 * OD].bitcast(FP8X4),
                lhsT_scale=head_scales[:, e, OD : 2 * OD],
                rhs=g_codes[i][:].bitcast(FP8X4),
                rhs_scale=g_scales[i][:],
                start=True,
                stop=True,
            )
            sigma_t[k] = keep.tile([P, COLS], F32, name="sg", tag="sg%d" % (k % HIT))
            nc.scalar.activation(
                out=sigma_t[k][:], in_=raw[:], func=ACT.Tanh, bias=sig_bias[:, e : e + 1], scale=1.0
            )

        def sigma_square(k):
            nc.gpsimd.tensor_scalar(
                out=sigma_t[k][:], in0=sigma_t[k][:], scalar1=slope[:], scalar2=offset[:],
                op0=ALU.mult, op1=ALU.add,
            )

        def sigma_out(k):
            c, e = divmod(k, E)
            back = bank(4 + k % 4, [P, SL, OD])
            for t in range(SL):
                nc.tensor.transpose(back[:, t, :], sigma_t[k][:, t * P : (t + 1) * P], ident_f[:])
            first, members = 0, E
            if c == CH - 1:
                first, members = (0, E - 1) if e < E - 1 else (E - 1, 1)
            if e == first:
                state[("sg", c)] = outs.tile([P, SL, members * SD], F32, name="ds_sg", tag="out")
            if e == 0:
                reward[("sg", c)] = work.tile([P, SL, E, RD], F32, name="r_sg", tag="reward", bufs=CH)
            nc.scalar.activation(
                out=state[("sg", c)][:, :, (e - first) * SD : (e - first + 1) * SD],
                in_=back[:, :, 0:SD], func=ACT.Sqrt,
            )
            nc.scalar.activation(out=reward[("sg", c)][:, :, e, :], in_=back[:, :, SD:OD], func=ACT.Sqrt)
            if e == first + members - 1:
                nc.sync.dma_start(
                    out=ds_sg_view[c][:, :, first * SD : (first + members) * SD], in_=state[("sg", c)][:]
                )
            if e == E - 1:
                nc.sync.dma_start(
                    out=r_sg_view[c], in_=reward[("sg", c)][:].rearrange("p t e o -> p (t e o)")
                )

        def prepare_bounds(bank_no):
            late_t = bank(bank_no, [P, P], BF16)
            nc.tensor.transpose(late_t[:], late[:], ident_b[:])
            nc.vector.tensor_copy(out=late_cols[:], in_=late_t[:, 0 : BOUND_ROW + 4])
            nc.vector.tensor_tensor(
                out=hi_lo[:], in0=late_cols[:, BOUND_ROW : BOUND_ROW + 2],
                in1=late_cols[:, BOUND_ROW + 2 : BOUND_ROW + 4], op=ALU.add,
            )
            nc.gpsimd.tensor_scalar(
                out=half_hi[:], in0=hi_lo[:, 0:1], scalar1=0.5, scalar2=0.0, op0=ALU.mult, op1=ALU.add
            )
            nc.gpsimd.tensor_scalar(
                out=log2_hi_lo[:], in0=hi_lo[:], scalar1=LOG2_E, scalar2=0.0, op0=ALU.mult, op1=ALU.add
            )
            nc.gpsimd.tensor_tensor(out=exp_hi_lo[:], in0=twos[:], in1=log2_hi_lo[:], op=ALU.pow)
            nc.gpsimd.tensor_scalar(
                out=slope[:], in0=exp_hi_lo[:, 0:1], scalar1=0.5, scalar2=0.0, op0=ALU.mult, op1=ALU.add
            )
            nc.gpsimd.tensor_tensor(out=offset[:], in0=slope[:], in1=exp_hi_lo[:, 1:2], op=ALU.add)

        def heads(half):
            first = half * HIT
            regroup_g(first + HIT - 1)
            following = first + HIT
            if following < NIT:
                copy_out(following)
                quantise_g(following - 1)
                copy_out(following + 1)
                quantise_h(following)
                for k in range(first, following):
                    sigma_head(k)
                    sigma_square(k)
                for step in range(4):
                    mu_head(len(mu_done))
            else:
                for k in range(first, first + 4):
                    sigma_head(k)
                    sigma_square(k)
                for step in range(4):
                    mu_head(len(mu_done))
                    if step == 0:
                        quantise_g(following - 1)
                for k in range(first + 4, following):
                    if k >= first + 10:
                        mu_head(len(mu_done))
                    sigma_head(k)
                    sigma_square(k)
            for k in range(first, following):
                if len(mu_done) < following:
                    mu_head(len(mu_done))
                sigma_out(k)
            if following < NIT:
                quantise_h(following + 1)
                for i in (following + 2, following + 3):
                    transposes(i, 0)
                    transposes(i, 1)
                    copy_out(i)
                layer(following)
                quantise_h(following + 2)
                for i in (following + 4, following + 5):
                    transposes(i, 0)
                    transposes(i, 1)
                    copy_out(i)

        load_weights(0)
        load_h(0)
        nc.sync.dma_start(out=early[0 : E * PACK, :], in_=bh.rearrange("e (j p) -> (e j) p", p=P))
        load_h(1)
        load_weights(1)
        load_h(2)
        load_weights(2)
        for i in range(3, H_SLOTS):
            load_h(i)
        regroup_weights(0)
        transposes(0, 0)
        transposes(0, 1)
        quantise_weights(0)
        copy_out(0)
        transposes(1, 0)
        transposes(1, 1)
        early_t = bank(7, [P, P], BF16)
        nc.tensor.transpose(early_t[:], early[:], ident_b[:])
        quantise_h(0)
        nc.vector.tensor_copy(out=early_cols[:], in_=early_t[:, 0 : E * PACK])
        copy_out(1)
        layer(0)
        for r in range(NIT):
            half, place = divmod(r, HIT)
            if r + AHEAD < NIT and (half == 0 or place + AHEAD >= 6):
                transposes(r + AHEAD, 0)
                transposes(r + AHEAD, 1)
            if place + 1 < HIT and (half == 0 or place > 1):
                quantise_h(r + 1)
            if r == HIT - 3:
                prepare_bounds(2 * ((r + 1) % 2))
            swish(r)
            if r + AHEAD == NIT:
                mu_head(len(mu_done))
            if place + 1 < HIT:
                layer(r + 1)
            if place > 0:
                regroup_g(r - 1)
            if r + 1 == NIT:
                mu_head(len(mu_done))
                mu_head(len(mu_done))
            if r // 2 + 1 < WEIGHT_SETS:
                if r % 2 == 0:
                    regroup_weights(r // 2 + 1)
                else:
                    quantise_weights(r // 2 + 1)
            if place + AHEAD < HIT and (half == 0 or place + AHEAD >= 6):
                copy_out(r + AHEAD)
            if place > 0:
                quantise_g(r - 1)
            if r == WEIGHT_SETS:
                nc.sync.dma_start(out=bmu_bf[:], in_=bmu.rearrange("e o -> (e o)").partition_broadcast(P))
                nc.sync.dma_start(out=late[0:E, :], in_=bsig)
                bounds = ((max_lv_s, 0, SD), (min_lv_s, 0, SD), (max_lv_r, SD, OD), (min_lv_r, SD, OD))
                for k, (bound, start, stop) in enumerate(bounds):
                    nc.sync.dma_start(out=late[BOUND_ROW + k : BOUND_ROW + k + 1, start:stop], in_=bound)
            if r == HIT - 3:
                nc.vector.tensor_copy(out=bmu_all[:], in_=bmu_bf[:])
                nc.vector.tensor_scalar(
                    out=sig_bias[:], in0=late_cols[:, 0:E], scalar1=half_hi[:], scalar2=None, op0=ALU.subtract
                )
            if place + 1 == HIT:
                heads(half)
